import numpy as np
import ml_dtypes


def mxq(x, axis, fmt="e4m3"):
    dtype, down = {"e4m3": (ml_dtypes.float8_e4m3fn, 7), "e5m2": (ml_dtypes.float8_e5m2, 14)}[fmt]
    v = np.moveaxis(np.asarray(x, np.float32).astype(ml_dtypes.bfloat16).astype(np.float64), axis, -1)
    blocks = v.reshape(v.shape[:-1] + (-1, 32))
    amax = np.abs(blocks).max(-1, keepdims=True)
    byte = np.maximum(np.where(amax > 0, np.frexp(amax)[1] - 1 + 127, 0) - down, 1)
    scale = np.exp2(byte - 127.0)
    codes = (blocks / scale).astype(np.float32).astype(dtype).astype(np.float64)
    return np.moveaxis((codes * scale).reshape(v.shape), -1, axis)


WIDE = False


def mx_kscale(k):
    if not WIDE:
        return np.ones(k)
    levels = np.array([10, -10, 5, -5, 0])
    a = np.random.permutation(np.resize(levels, k // 512 * 4)).reshape(k // 512, 4)
    idx = np.arange(k)
    return np.exp2(a[idx // 512, idx % 128 // 32])


BF16 = ml_dtypes.bfloat16


def bf(x):
    return np.asarray(x, np.float32).astype(BF16)


def f64(x):
    return np.asarray(x).astype(np.float64)


B, I, H = 4096, 256, 512


def setup_inputs():
    s = mx_kscale(H)
    w1 = np.concatenate([np.random.standard_normal((H, H)) * 1.5 / np.sqrt(H) / s, np.random.standard_normal(H)[:, None] * 0.6], axis=1)
    return {"h_tilde": bf(np.random.standard_normal((B, H)) * 0.3 * s),
            "k_prev": bf(np.random.standard_normal((B, H)) * 0.9 * s),
            "t0": bf(0.2 + 0.1 * np.random.random(1)),
            "t1": bf(1.0 + 0.2 * np.random.random(1)),
            "W1": bf(w1),
            "b1": bf(np.random.standard_normal(H) * 0.3),
            "W2": bf(np.random.standard_normal((H, H)) * 1.5 / np.sqrt(H)),
            "b2": bf(np.random.standard_normal(H) * 0.3)}


def reference(h_tilde, k_prev, t0, t1, W1, b1, W2, b2):
    dt = f64(t1) - f64(t0)
    t = f64(t0) + 0.5 * dt
    y = f64(h_tilde) + 0.5 * dt * f64(k_prev)
    w1 = f64(W1)
    z = np.tanh((mxq(y, 1, "e4m3") @ mxq(w1[:, :H], 1, "e4m3").T) + t * w1[:, H] + f64(b1))
    return (mxq(z, 1, "e4m3") @ mxq(f64(W2), 1, "e4m3").T) + f64(b2)

@@ -1,0 +1,184 @@
+from contextlib import ExitStack
+
+import concourse.mybir as mybir
+from concourse.masks import make_identity
+
+BF16 = mybir.dt.bfloat16
+F32 = mybir.dt.float32
+U32 = mybir.dt.uint32
+U8 = mybir.dt.uint8
+FP8X4 = mybir.dt.float8_e4m3fn_x4
+ALU = mybir.AluOpType
+ACT = mybir.ActivationFunctionType
+
+P = 128
+PACK = 4
+WIDTH = P * PACK
+BATCH = 4096
+N_CHUNKS = BATCH // WIDTH
+HALF = WIDTH // 2
+
+Z_COLS_ON_VECTOR = 128
+
+FLOPS = 2 * 2 * BATCH * WIDTH * WIDTH
+
+
+def tile_nodelstmcell_pb_t_kernel(tc, h_tilde, k_prev, t0, t1, W1, b1, W2, b2, out):
+    nc = tc.nc
+
+    h_chunks = h_tilde.rearrange("(c q s) k -> c q s k", q=P, s=PACK)
+    k_chunks = k_prev.rearrange("(c q s) k -> c q s k", q=P, s=PACK)
+    out_chunks = out.rearrange("(c q s) n -> c q s n", q=P, s=PACK)
+
+    with ExitStack() as ctx:
+        const = ctx.enter_context(tc.tile_pool(name="const", bufs=1))
+        inputs = ctx.enter_context(tc.tile_pool(name="inputs", bufs=N_CHUNKS))
+        work = ctx.enter_context(tc.tile_pool(name="work", bufs=3))
+        turned_banks = ctx.enter_context(tc.psum_pool(name="turned_banks", bufs=2))
+        hidden_banks = ctx.enter_context(tc.psum_pool(name="hidden_banks", bufs=3))
+        out_banks = ctx.enter_context(tc.psum_pool(name="out_banks", bufs=3))
+
+        identity = const.tile([P, P], BF16)
+        make_identity(nc, identity[:])
+
+        def quantise_rows(rows, codes, scales):
+            grouped = work.tile([P, WIDTH, PACK], BF16, align_bytes=64)
+            for half in range(2):
+                turned = turned_banks.tile([P, PACK, HALF], BF16)
+                for s in range(2):
+                    for t in range(PACK):
+                        nc.tensor.transpose(
+                            turned[:, t, s * P : (s + 1) * P],
+                            rows[:, 2 * half + s, t * P : (t + 1) * P],
+                            identity[:],
+                        )
+                nc.scalar.copy(
+                    out=grouped[:, half * HALF : (half + 1) * HALF, :],
+                    in_=turned[:].rearrange("p t c -> p c t"),
+                )
+            nc.vector.quantize_mx(
+                out=codes.bitcast(FP8X4),
+                scales=scales,
+                in_=grouped[:].rearrange("p c t -> p (c t)"),
+            )
+
+        t0_all = const.tile([P, 1], BF16)
+        t1_all = const.tile([P, 1], BF16)
+        nc.scalar.dma_start(out=t0_all[:], in_=t0.partition_broadcast(P))
+        nc.scalar.dma_start(out=t1_all[:], in_=t1.partition_broadcast(P))
+
+        b1_rows = const.tile([P, P], BF16)
+        nc.vector.memset(b1_rows[:], 0.0)
+        nc.scalar.dma_start(out=b1_rows[0:PACK, :], in_=b1.rearrange("(r m) -> r m", m=P))
+
+        h_rows = []
+        k_rows = []
+        for c in range(N_CHUNKS):
+            h_rows.append(inputs.tile([P, PACK, WIDTH], BF16, name="h_rows"))
+            k_rows.append(inputs.tile([P, PACK, WIDTH], BF16, name="k_rows"))
+
+        def load_chunk(c):
+            nc.sync.dma_start(out=h_rows[c][:], in_=h_chunks[c])
+            nc.sync.dma_start(out=k_rows[c][:], in_=k_chunks[c])
+
+        w1_rows = const.tile([P, PACK, WIDTH + 2], BF16)
+        w2_rows = const.tile([P, PACK, WIDTH], BF16)
+        b2_all = const.tile([P, WIDTH], BF16)
+
+        load_chunk(0)
+        nc.sync.dma_start(
+            out=w1_rows[:, :, 0 : WIDTH + 1], in_=W1.rearrange("(r m) k -> m r k", m=P)
+        )
+        load_chunk(1)
+        nc.sync.dma_start(out=w2_rows[:], in_=W2.rearrange("(r m) k -> m r k", m=P))
+        nc.sync.dma_start(out=b2_all[:], in_=b2.partition_broadcast(P))
+        for c in range(2, N_CHUNKS):
+            load_chunk(c)
+
+        half_dt = const.tile([P, 1], F32)
+        t_mid = const.tile([P, 1], F32)
+        nc.vector.tensor_sub(out=half_dt[:], in0=t1_all[:], in1=t0_all[:])
+        nc.vector.tensor_scalar_mul(out=half_dt[:], in0=half_dt[:], scalar1=0.5)
+        nc.vector.tensor_add(out=t_mid[:], in0=t0_all[:], in1=half_dt[:])
+
+        w1_codes = const.tile([P, WIDTH], U32, align_bytes=64)
+        w1_scales = const.tile([P, WIDTH], U8, align_bytes=64)
+        w2_codes = const.tile([P, WIDTH], U32, align_bytes=64)
+        w2_scales = const.tile([P, WIDTH], U8, align_bytes=64)
+        quantise_rows(w1_rows, w1_codes[:], w1_scales[:])
+
+        b1_turned = turned_banks.tile([P, PACK, HALF], BF16, name="turned")
+        nc.tensor.transpose(b1_turned[:, 0, 0:P], b1_rows[:], identity[:])
+        bias1 = const.tile([P, PACK], F32)
+        nc.vector.scalar_tensor_tensor(
+            out=bias1[:],
+            in0=w1_rows[:, :, WIDTH],
+            scalar=t_mid[:, 0:1],
+            in1=b1_turned[:, 0, 0:PACK],
+            op0=ALU.mult,
+            op1=ALU.add,
+        )
+        quantise_rows(w2_rows, w2_codes[:], w2_scales[:])
+
+        for c in range(N_CHUNKS):
+            y_rows = work.tile([P, PACK, WIDTH], BF16)
+            nc.vector.scalar_tensor_tensor(
+                out=y_rows[:],
+                in0=k_rows[c][:],
+                scalar=half_dt[:, 0:1],
+                in1=h_rows[c][:],
+                op0=ALU.mult,
+                op1=ALU.add,
+            )
+            y_codes = work.tile([P, WIDTH], U32, align_bytes=64)
+            y_scales = work.tile([P, WIDTH], U8, align_bytes=64)
+            quantise_rows(y_rows, y_codes[:], y_scales[:])
+
+            z_planes = work.tile([P, PACK, WIDTH], BF16)
+            for r in range(PACK):
+                hidden = hidden_banks.tile([P, WIDTH], F32)
+                nc.tensor.matmul_mx(
+                    out=hidden[:],
+                    lhsT=w1_codes[:, r * P : (r + 1) * P].bitcast(FP8X4),
+                    lhsT_scale=w1_scales[:, r * P : (r + 1) * P],
+                    rhs=y_codes[:].bitcast(FP8X4),
+                    rhs_scale=y_scales[:],
+                    start=True,
+                    stop=True,
+                )
+                nc.scalar.activation(
+                    out=z_planes[:, r, :], in_=hidden[:], func=ACT.Tanh, bias=bias1[:, r : r + 1]
+                )
+
+            z_grouped = work.tile([P, WIDTH, PACK], BF16, align_bytes=64)
+            split = Z_COLS_ON_VECTOR
+            nc.vector.tensor_copy(
+                out=z_grouped[:, 0:split, :].rearrange("p (c i) t -> p c t i", i=4),
+                in_=z_planes[:, :, 0:split].rearrange("p t (c i) -> p c t i", i=4),
+            )
+            nc.scalar.copy(
+                out=z_grouped[:, split:WIDTH, :].rearrange("p (c i) t -> p c t i", i=4),
+                in_=z_planes[:, :, split:WIDTH].rearrange("p t (c i) -> p c t i", i=4),
+            )
+            z_codes = work.tile([P, WIDTH], U32, align_bytes=64)
+            z_scales = work.tile([P, WIDTH], U8, align_bytes=64)
+            nc.vector.quantize_mx(
+                out=z_codes[:].bitcast(FP8X4),
+                scales=z_scales[:],
+                in_=z_grouped[:].rearrange("p c t -> p (c t)"),
+            )
+
+            result = work.tile([P, PACK, WIDTH], F32)
+            for s in range(PACK):
+                summed = out_banks.tile([P, WIDTH], F32)
+                nc.tensor.matmul_mx(
+                    out=summed[:],
+                    lhsT=z_codes[:, s * P : (s + 1) * P].bitcast(FP8X4),
+                    lhsT_scale=z_scales[:, s * P : (s + 1) * P],
+                    rhs=w2_codes[:].bitcast(FP8X4),
+                    rhs_scale=w2_scales[:],
+                    start=True,
+                    stop=True,
+                )
+                nc.vector.tensor_add(out=result[:, s, :], in0=summed[:], in1=b2_all[:])
+            nc.sync.dma_start(out=out_chunks[c], in_=result[:])

@@ -16,9 +16,9 @@ PACK = 4
 WIDTH = P * PACK
 BATCH = 4096
 N_CHUNKS = BATCH // WIDTH
-HALF = WIDTH // 2
+BANK_COLS = 256
 
-Z_COLS_ON_VECTOR = 128
+Z_COLS_ON_VECTOR = 256
 
 FLOPS = 2 * 2 * BATCH * WIDTH * WIDTH
 
@@ -31,20 +31,49 @@ def tile_nodelstmcell_pb_t_kernel(tc, h_tilde, k_prev, t0, t1, W1, b1, W2, b2, o
     out_chunks = out.rearrange("(c q s) n -> c q s n", q=P, s=PACK)
 
     with ExitStack() as ctx:
+        ctx.enter_context(tc.manual_schedule())
         const = ctx.enter_context(tc.tile_pool(name="const", bufs=1))
         inputs = ctx.enter_context(tc.tile_pool(name="inputs", bufs=N_CHUNKS))
-        work = ctx.enter_context(tc.tile_pool(name="work", bufs=3))
+        work = ctx.enter_context(tc.tile_pool(name="work", bufs=4))
         turned_banks = ctx.enter_context(tc.psum_pool(name="turned_banks", bufs=2))
-        hidden_banks = ctx.enter_context(tc.psum_pool(name="hidden_banks", bufs=3))
-        out_banks = ctx.enter_context(tc.psum_pool(name="out_banks", bufs=3))
+        hidden_banks = ctx.enter_context(tc.psum_pool(name="hidden_banks", bufs=2))
+        out_banks = ctx.enter_context(tc.psum_pool(name="out_banks", bufs=PACK))
+
+        t0_all = const.tile([P, 1], BF16)
+        t1_all = const.tile([P, 1], BF16)
+        nc.scalar.dma_start(out=t0_all[:], in_=t0.partition_broadcast(P))
+        nc.scalar.dma_start(out=t1_all[:], in_=t1.partition_broadcast(P))
+        b1_rows = const.tile([P, P], BF16)
+        nc.vector.memset(b1_rows[:], 0.0)
+        nc.scalar.dma_start(out=b1_rows[0:PACK, :], in_=b1.rearrange("(r m) -> r m", m=P))
+
+        w1_rows = const.tile([P, PACK, WIDTH + 2], BF16)
+        w2_rows = const.tile([P, PACK, WIDTH], BF16)
+        b2_all = const.tile([P, WIDTH], BF16)
+        h_rows = []
+        k_rows = []
+        nc.sync.dma_start(
+            out=w1_rows[:, :, 0 : WIDTH + 1], in_=W1.rearrange("(r m) k -> m r k", m=P)
+        )
+        nc.sync.dma_start(out=w2_rows[:], in_=W2.rearrange("(r m) k -> m r k", m=P))
+        for c in range(N_CHUNKS):
+            h_rows.append(inputs.tile([P, PACK, WIDTH], BF16, name="h_rows"))
+            k_rows.append(inputs.tile([P, PACK, WIDTH], BF16, name="k_rows"))
+            nc.sync.dma_start(out=h_rows[c][:], in_=h_chunks[c])
+            nc.sync.dma_start(out=k_rows[c][:], in_=k_chunks[c])
+        nc.sync.dma_start(out=b2_all[:], in_=b2.partition_broadcast(P))
 
         identity = const.tile([P, P], BF16)
         make_identity(nc, identity[:])
 
-        def quantise_rows(rows, codes, scales):
+        warm = const.tile([P, 1], F32)
+        nc.vector.memset(warm[:], 0.0)
+        nc.scalar.activation(out=warm[:], in_=warm[:], func=ACT.Tanh)
+
+        def turn(rows):
             grouped = work.tile([P, WIDTH, PACK], BF16, align_bytes=64)
             for half in range(2):
-                turned = turned_banks.tile([P, PACK, HALF], BF16)
+                turned = turned_banks.tile([P, PACK, BANK_COLS], BF16)
                 for s in range(2):
                     for t in range(PACK):
                         nc.tensor.transpose(
@@ -53,47 +82,31 @@ def tile_nodelstmcell_pb_t_kernel(tc, h_tilde, k_prev, t0, t1, W1, b1, W2, b2, o
                             identity[:],
                         )
                 nc.scalar.copy(
-                    out=grouped[:, half * HALF : (half + 1) * HALF, :],
+                    out=grouped[:, half * BANK_COLS : (half + 1) * BANK_COLS, :],
                     in_=turned[:].rearrange("p t c -> p c t"),
                 )
+            return grouped
+
+        def quantise(grouped, pool, name):
+            codes = pool.tile([P, WIDTH], U32, align_bytes=64, name=name + "_codes")
+            scales = pool.tile([P, WIDTH], U8, align_bytes=64, name=name + "_scales")
             nc.vector.quantize_mx(
-                out=codes.bitcast(FP8X4),
-                scales=scales,
+                out=codes[:].bitcast(FP8X4),
+                scales=scales[:],
                 in_=grouped[:].rearrange("p c t -> p (c t)"),
             )
+            return codes, scales
 
-        t0_all = const.tile([P, 1], BF16)
-        t1_all = const.tile([P, 1], BF16)
-        nc.scalar.dma_start(out=t0_all[:], in_=t0.partition_broadcast(P))
-        nc.scalar.dma_start(out=t1_all[:], in_=t1.partition_broadcast(P))
-
-        b1_rows = const.tile([P, P], BF16)
-        nc.vector.memset(b1_rows[:], 0.0)
-        nc.scalar.dma_start(out=b1_rows[0:PACK, :], in_=b1.rearrange("(r m) -> r m", m=P))
-
-        h_rows = []
-        k_rows = []
-        for c in range(N_CHUNKS):
-            h_rows.append(inputs.tile([P, PACK, WIDTH], BF16, name="h_rows"))
-            k_rows.append(inputs.tile([P, PACK, WIDTH], BF16, name="k_rows"))
-
-        def load_chunk(c):
-            nc.sync.dma_start(out=h_rows[c][:], in_=h_chunks[c])
-            nc.sync.dma_start(out=k_rows[c][:], in_=k_chunks[c])
-
-        w1_rows = const.tile([P, PACK, WIDTH + 2], BF16)
-        w2_rows = const.tile([P, PACK, WIDTH], BF16)
-        b2_all = const.tile([P, WIDTH], BF16)
-
-        load_chunk(0)
-        nc.sync.dma_start(
-            out=w1_rows[:, :, 0 : WIDTH + 1], in_=W1.rearrange("(r m) k -> m r k", m=P)
-        )
-        load_chunk(1)
-        nc.sync.dma_start(out=w2_rows[:], in_=W2.rearrange("(r m) k -> m r k", m=P))
-        nc.sync.dma_start(out=b2_all[:], in_=b2.partition_broadcast(P))
-        for c in range(2, N_CHUNKS):
-            load_chunk(c)
+        def multiply(acc, stationary, columns, moving):
+            nc.tensor.matmul_mx(
+                out=acc[:],
+                lhsT=stationary[0][:, columns].bitcast(FP8X4),
+                lhsT_scale=stationary[1][:, columns],
+                rhs=moving[0][:].bitcast(FP8X4),
+                rhs_scale=moving[1][:],
+                start=True,
+                stop=True,
+            )
 
         half_dt = const.tile([P, 1], F32)
         t_mid = const.tile([P, 1], F32)
@@ -101,13 +114,7 @@ def tile_nodelstmcell_pb_t_kernel(tc, h_tilde, k_prev, t0, t1, W1, b1, W2, b2, o
         nc.vector.tensor_scalar_mul(out=half_dt[:], in0=half_dt[:], scalar1=0.5)
         nc.vector.tensor_add(out=t_mid[:], in0=t0_all[:], in1=half_dt[:])
 
-        w1_codes = const.tile([P, WIDTH], U32, align_bytes=64)
-        w1_scales = const.tile([P, WIDTH], U8, align_bytes=64)
-        w2_codes = const.tile([P, WIDTH], U32, align_bytes=64)
-        w2_scales = const.tile([P, WIDTH], U8, align_bytes=64)
-        quantise_rows(w1_rows, w1_codes[:], w1_scales[:])
-
-        b1_turned = turned_banks.tile([P, PACK, HALF], BF16, name="turned")
+        b1_turned = turned_banks.tile([P, PACK, BANK_COLS], BF16, name="turned")
         nc.tensor.transpose(b1_turned[:, 0, 0:P], b1_rows[:], identity[:])
         bias1 = const.tile([P, PACK], F32)
         nc.vector.scalar_tensor_tensor(
@@ -118,9 +125,13 @@ def tile_nodelstmcell_pb_t_kernel(tc, h_tilde, k_prev, t0, t1, W1, b1, W2, b2, o
             op0=ALU.mult,
             op1=ALU.add,
         )
-        quantise_rows(w2_rows, w2_codes[:], w2_scales[:])
 
-        for c in range(N_CHUNKS):
+        y_grouped = {}
+        z_planes = {}
+        z_grouped = {}
+        sums = {}
+
+        def combine_and_turn(c):
             y_rows = work.tile([P, PACK, WIDTH], BF16)
             nc.vector.scalar_tensor_tensor(
                 out=y_rows[:],
@@ -130,55 +141,52 @@ def tile_nodelstmcell_pb_t_kernel(tc, h_tilde, k_prev, t0, t1, W1, b1, W2, b2, o
                 op0=ALU.mult,
                 op1=ALU.add,
             )
-            y_codes = work.tile([P, WIDTH], U32, align_bytes=64)
-            y_scales = work.tile([P, WIDTH], U8, align_bytes=64)
-            quantise_rows(y_rows, y_codes[:], y_scales[:])
+            y_grouped[c] = turn(y_rows)
 
-            z_planes = work.tile([P, PACK, WIDTH], BF16)
+        def lay_out_z(copy, c, first, last):
+            copy(
+                out=z_grouped[c][:, first:last, :].rearrange("p (c i) t -> p c t i", i=4),
+                in_=z_planes[c][:, :, first:last].rearrange("p t (c i) -> p c t i", i=4),
+            )
+
+        def first_layer(c):
+            y_mx = quantise(y_grouped[c], work, "y")
+            z_planes[c] = work.tile([P, PACK, WIDTH], BF16, name="z_planes")
+            z_grouped[c] = work.tile([P, WIDTH, PACK], BF16, align_bytes=64, name="z_grouped")
             for r in range(PACK):
                 hidden = hidden_banks.tile([P, WIDTH], F32)
-                nc.tensor.matmul_mx(
-                    out=hidden[:],
-                    lhsT=w1_codes[:, r * P : (r + 1) * P].bitcast(FP8X4),
-                    lhsT_scale=w1_scales[:, r * P : (r + 1) * P],
-                    rhs=y_codes[:].bitcast(FP8X4),
-                    rhs_scale=y_scales[:],
-                    start=True,
-                    stop=True,
-                )
+                multiply(hidden, w1_mx, slice(r * P, (r + 1) * P), y_mx)
                 nc.scalar.activation(
-                    out=z_planes[:, r, :], in_=hidden[:], func=ACT.Tanh, bias=bias1[:, r : r + 1]
+                    out=z_planes[c][:, r, :], in_=hidden[:], func=ACT.Tanh, bias=bias1[:, r : r + 1]
                 )
+            lay_out_z(nc.scalar.copy, c, Z_COLS_ON_VECTOR, WIDTH)
 
-            z_grouped = work.tile([P, WIDTH, PACK], BF16, align_bytes=64)
-            split = Z_COLS_ON_VECTOR
-            nc.vector.tensor_copy(
-                out=z_grouped[:, 0:split, :].rearrange("p (c i) t -> p c t i", i=4),
-                in_=z_planes[:, :, 0:split].rearrange("p t (c i) -> p c t i", i=4),
-            )
-            nc.scalar.copy(
-                out=z_grouped[:, split:WIDTH, :].rearrange("p (c i) t -> p c t i", i=4),
-                in_=z_planes[:, :, split:WIDTH].rearrange("p t (c i) -> p c t i", i=4),
-            )
-            z_codes = work.tile([P, WIDTH], U32, align_bytes=64)
-            z_scales = work.tile([P, WIDTH], U8, align_bytes=64)
-            nc.vector.quantize_mx(
-                out=z_codes[:].bitcast(FP8X4),
-                scales=z_scales[:],
-                in_=z_grouped[:].rearrange("p c t -> p (c t)"),
-            )
-
-            result = work.tile([P, PACK, WIDTH], F32)
+        def pack_hidden(c):
+            lay_out_z(nc.vector.tensor_copy, c, 0, Z_COLS_ON_VECTOR)
+            z_mx = quantise(z_grouped[c], work, "z")
+            sums[c] = []
             for s in range(PACK):
                 summed = out_banks.tile([P, WIDTH], F32)
-                nc.tensor.matmul_mx(
-                    out=summed[:],
-                    lhsT=z_codes[:, s * P : (s + 1) * P].bitcast(FP8X4),
-                    lhsT_scale=z_scales[:, s * P : (s + 1) * P],
-                    rhs=w2_codes[:].bitcast(FP8X4),
-                    rhs_scale=w2_scales[:],
-                    start=True,
-                    stop=True,
-                )
-                nc.vector.tensor_add(out=result[:, s, :], in0=summed[:], in1=b2_all[:])
-            nc.sync.dma_start(out=out_chunks[c], in_=result[:])
+                multiply(summed, z_mx, slice(s * P, (s + 1) * P), w2_mx)
+                sums[c].append(summed)
+
+        def finish(c):
+            result = work.tile([P, PACK, WIDTH], F32)
+            for s in range(PACK):
+                nc.vector.tensor_add(out=result[:, s, :], in0=sums[c][s][:], in1=b2_all[:])
+                nc.sync.dma_start(out=out_chunks[c][:, s, :], in_=result[:, s, :])
+
+        def run(stage, c):
+            if 0 <= c < N_CHUNKS:
+                stage(c)
+
+        w1_grouped = turn(w1_rows)
+        w2_grouped = turn(w2_rows)
+        w1_mx = quantise(w1_grouped, const, "w1")
+        combine_and_turn(0)
+        w2_mx = quantise(w2_grouped, const, "w2")
+        for step in range(1, N_CHUNKS + 5):
+            run(finish, step - 5)
+            run(pack_hidden, step - 4)
+            run(first_layer, step - 2)
+            run(combine_and_turn, step)

@@ -35,9 +35,8 @@ def tile_nodelstmcell_pb_t_kernel(tc, h_tilde, k_prev, t0, t1, W1, b1, W2, b2, o
         const = ctx.enter_context(tc.tile_pool(name="const", bufs=1))
         inputs = ctx.enter_context(tc.tile_pool(name="inputs", bufs=N_CHUNKS))
         work = ctx.enter_context(tc.tile_pool(name="work", bufs=4))
-        turned_banks = ctx.enter_context(tc.psum_pool(name="turned_banks", bufs=2))
-        hidden_banks = ctx.enter_context(tc.psum_pool(name="hidden_banks", bufs=2))
-        out_banks = ctx.enter_context(tc.psum_pool(name="out_banks", bufs=PACK))
+        scalar_banks = ctx.enter_context(tc.psum_pool(name="scalar_banks", bufs=4))
+        vector_banks = ctx.enter_context(tc.psum_pool(name="vector_banks", bufs=PACK))
 
         t0_all = const.tile([P, 1], BF16)
         t1_all = const.tile([P, 1], BF16)
@@ -55,12 +54,13 @@ def tile_nodelstmcell_pb_t_kernel(tc, h_tilde, k_prev, t0, t1, W1, b1, W2, b2, o
         nc.sync.dma_start(
             out=w1_rows[:, :, 0 : WIDTH + 1], in_=W1.rearrange("(r m) k -> m r k", m=P)
         )
-        nc.sync.dma_start(out=w2_rows[:], in_=W2.rearrange("(r m) k -> m r k", m=P))
         for c in range(N_CHUNKS):
             h_rows.append(inputs.tile([P, PACK, WIDTH], BF16, name="h_rows"))
             k_rows.append(inputs.tile([P, PACK, WIDTH], BF16, name="k_rows"))
             nc.sync.dma_start(out=h_rows[c][:], in_=h_chunks[c])
             nc.sync.dma_start(out=k_rows[c][:], in_=k_chunks[c])
+            if c == 0:
+                nc.sync.dma_start(out=w2_rows[:], in_=W2.rearrange("(r m) k -> m r k", m=P))
         nc.sync.dma_start(out=b2_all[:], in_=b2.partition_broadcast(P))
 
         identity = const.tile([P, P], BF16)
@@ -73,7 +73,7 @@ def tile_nodelstmcell_pb_t_kernel(tc, h_tilde, k_prev, t0, t1, W1, b1, W2, b2, o
         def turn(rows):
             grouped = work.tile([P, WIDTH, PACK], BF16, align_bytes=64)
             for half in range(2):
-                turned = turned_banks.tile([P, PACK, BANK_COLS], BF16)
+                turned = scalar_banks.tile([P, PACK, BANK_COLS], BF16, tag="bank")
                 for s in range(2):
                     for t in range(PACK):
                         nc.tensor.transpose(
@@ -114,18 +114,6 @@ def tile_nodelstmcell_pb_t_kernel(tc, h_tilde, k_prev, t0, t1, W1, b1, W2, b2, o
         nc.vector.tensor_scalar_mul(out=half_dt[:], in0=half_dt[:], scalar1=0.5)
         nc.vector.tensor_add(out=t_mid[:], in0=t0_all[:], in1=half_dt[:])
 
-        b1_turned = turned_banks.tile([P, PACK, BANK_COLS], BF16, name="turned")
-        nc.tensor.transpose(b1_turned[:, 0, 0:P], b1_rows[:], identity[:])
-        bias1 = const.tile([P, PACK], F32)
-        nc.vector.scalar_tensor_tensor(
-            out=bias1[:],
-            in0=w1_rows[:, :, WIDTH],
-            scalar=t_mid[:, 0:1],
-            in1=b1_turned[:, 0, 0:PACK],
-            op0=ALU.mult,
-            op1=ALU.add,
-        )
-
         y_grouped = {}
         z_planes = {}
         z_grouped = {}
@@ -154,39 +142,53 @@ def tile_nodelstmcell_pb_t_kernel(tc, h_tilde, k_prev, t0, t1, W1, b1, W2, b2, o
             z_planes[c] = work.tile([P, PACK, WIDTH], BF16, name="z_planes")
             z_grouped[c] = work.tile([P, WIDTH, PACK], BF16, align_bytes=64, name="z_grouped")
             for r in range(PACK):
-                hidden = hidden_banks.tile([P, WIDTH], F32)
+                hidden = scalar_banks.tile([P, WIDTH], F32, tag="bank")
                 multiply(hidden, w1_mx, slice(r * P, (r + 1) * P), y_mx)
                 nc.scalar.activation(
                     out=z_planes[c][:, r, :], in_=hidden[:], func=ACT.Tanh, bias=bias1[:, r : r + 1]
                 )
             lay_out_z(nc.scalar.copy, c, Z_COLS_ON_VECTOR, WIDTH)
 
-        def pack_hidden(c):
-            lay_out_z(nc.vector.tensor_copy, c, 0, Z_COLS_ON_VECTOR)
-            z_mx = quantise(z_grouped[c], work, "z")
-            sums[c] = []
+        def second_layer(c):
+            if c < N_CHUNKS:
+                lay_out_z(nc.vector.tensor_copy, c, 0, Z_COLS_ON_VECTOR)
+                sums[c] = []
+            if c > 0:
+                result = work.tile([P, PACK, WIDTH], F32)
             for s in range(PACK):
-                summed = out_banks.tile([P, WIDTH], F32)
-                multiply(summed, z_mx, slice(s * P, (s + 1) * P), w2_mx)
-                sums[c].append(summed)
-
-        def finish(c):
-            result = work.tile([P, PACK, WIDTH], F32)
-            for s in range(PACK):
-                nc.vector.tensor_add(out=result[:, s, :], in0=sums[c][s][:], in1=b2_all[:])
-                nc.sync.dma_start(out=out_chunks[c][:, s, :], in_=result[:, s, :])
-
-        def run(stage, c):
-            if 0 <= c < N_CHUNKS:
-                stage(c)
+                if c > 0:
+                    nc.vector.tensor_add(out=result[:, s, :], in0=sums[c - 1][s][:], in1=b2_all[:])
+                    nc.sync.dma_start(out=out_chunks[c - 1][:, s, :], in_=result[:, s, :])
+                if c < N_CHUNKS:
+                    if s == 0:
+                        z_mx = quantise(z_grouped[c], work, "z")
+                    summed = vector_banks.tile([P, WIDTH], F32)
+                    multiply(summed, z_mx, slice(s * P, (s + 1) * P), w2_mx)
+                    sums[c].append(summed)
 
         w1_grouped = turn(w1_rows)
         w2_grouped = turn(w2_rows)
-        w1_mx = quantise(w1_grouped, const, "w1")
         combine_and_turn(0)
+        w1_mx = quantise(w1_grouped, const, "w1")
+
+        b1_turned = scalar_banks.tile([P, PACK, BANK_COLS], BF16, tag="bank")
+        nc.tensor.transpose(b1_turned[:, 0, 0:P], b1_rows[:], identity[:])
+        bias1 = const.tile([P, PACK], F32)
+        nc.vector.scalar_tensor_tensor(
+            out=bias1[:],
+            in0=w1_rows[:, :, WIDTH],
+            scalar=t_mid[:, 0:1],
+            in1=b1_turned[:, 0, 0:PACK],
+            op0=ALU.mult,
+            op1=ALU.add,
+        )
+
+        combine_and_turn(1)
         w2_mx = quantise(w2_grouped, const, "w2")
-        for step in range(1, N_CHUNKS + 5):
-            run(finish, step - 5)
-            run(pack_hidden, step - 4)
-            run(first_layer, step - 2)
-            run(combine_and_turn, step)
+        for step in range(2, N_CHUNKS + 5):
+            if step >= 4:
+                second_layer(step - 4)
+            if step - 2 < N_CHUNKS:
+                first_layer(step - 2)
+            if step < N_CHUNKS:
+                combine_and_turn(step)

@@ -17,6 +17,7 @@ WIDTH = P * PACK
 BATCH = 4096
 N_CHUNKS = BATCH // WIDTH
 BANK_COLS = 256
+TIME_STEP = 16
 
 Z_COLS_ON_VECTOR = 256
 
@@ -38,17 +39,21 @@ def tile_nodelstmcell_pb_t_kernel(tc, h_tilde, k_prev, t0, t1, W1, b1, W2, b2, o
         scalar_banks = ctx.enter_context(tc.psum_pool(name="scalar_banks", bufs=4))
         vector_banks = ctx.enter_context(tc.psum_pool(name="vector_banks", bufs=PACK))
 
-        t0_all = const.tile([P, 1], BF16)
-        t1_all = const.tile([P, 1], BF16)
-        nc.scalar.dma_start(out=t0_all[:], in_=t0.partition_broadcast(P))
-        nc.scalar.dma_start(out=t1_all[:], in_=t1.partition_broadcast(P))
+        times_row = const.tile([P, 2 * TIME_STEP], BF16)
+        nc.vector.memset(times_row[:], 0.0)
+        nc.scalar.dma_start(out=times_row[0:1, 0:1], in_=t0.rearrange("(o n) -> o n", o=1))
+        nc.scalar.dma_start(
+            out=times_row[0:1, TIME_STEP : TIME_STEP + 1], in_=t1.rearrange("(o n) -> o n", o=1)
+        )
+        b2_row = const.tile([P, WIDTH], BF16)
+        nc.vector.memset(b2_row[:], 0.0)
+        nc.scalar.dma_start(out=b2_row[0:1, :], in_=b2.rearrange("(o n) -> o n", o=1))
         b1_rows = const.tile([P, P], BF16)
         nc.vector.memset(b1_rows[:], 0.0)
         nc.scalar.dma_start(out=b1_rows[0:PACK, :], in_=b1.rearrange("(r m) -> r m", m=P))
 
         w1_rows = const.tile([P, PACK, WIDTH + 2], BF16)
         w2_rows = const.tile([P, PACK, WIDTH], BF16)
-        b2_all = const.tile([P, WIDTH], BF16)
         h_rows = []
         k_rows = []
         nc.sync.dma_start(
@@ -61,7 +66,6 @@ def tile_nodelstmcell_pb_t_kernel(tc, h_tilde, k_prev, t0, t1, W1, b1, W2, b2, o
             nc.sync.dma_start(out=k_rows[c][:], in_=k_chunks[c])
             if c == 0:
                 nc.sync.dma_start(out=w2_rows[:], in_=W2.rearrange("(r m) k -> m r k", m=P))
-        nc.sync.dma_start(out=b2_all[:], in_=b2.partition_broadcast(P))
 
         identity = const.tile([P, P], BF16)
         make_identity(nc, identity[:])
@@ -108,11 +112,25 @@ def tile_nodelstmcell_pb_t_kernel(tc, h_tilde, k_prev, t0, t1, W1, b1, W2, b2, o
                 stop=True,
             )
 
+        ones = const.tile([P, P], BF16)
+        nc.vector.memset(ones[:], 1.0)
+
+        def spread(row, name):
+            width = row.shape[1]
+            bank = scalar_banks.tile([P, WIDTH], F32, tag="bank")
+            nc.tensor.matmul(out=bank[:, 0:width], lhsT=ones[:], rhs=row[:], start=True, stop=True)
+            everywhere = const.tile([P, width], F32, name=name)
+            nc.vector.tensor_copy(out=everywhere[:], in_=bank[:, 0:width])
+            return everywhere
+
+        times = spread(times_row, "times")
+        t0_all = times[:, 0:1]
+        t1_all = times[:, TIME_STEP : TIME_STEP + 1]
         half_dt = const.tile([P, 1], F32)
         t_mid = const.tile([P, 1], F32)
-        nc.vector.tensor_sub(out=half_dt[:], in0=t1_all[:], in1=t0_all[:])
+        nc.vector.tensor_sub(out=half_dt[:], in0=t1_all, in1=t0_all)
         nc.vector.tensor_scalar_mul(out=half_dt[:], in0=half_dt[:], scalar1=0.5)
-        nc.vector.tensor_add(out=t_mid[:], in0=t0_all[:], in1=half_dt[:])
+        nc.vector.tensor_add(out=t_mid[:], in0=t0_all, in1=half_dt[:])
 
         y_grouped = {}
         z_planes = {}
@@ -147,7 +165,6 @@ def tile_nodelstmcell_pb_t_kernel(tc, h_tilde, k_prev, t0, t1, W1, b1, W2, b2, o
                 nc.scalar.activation(
                     out=z_planes[c][:, r, :], in_=hidden[:], func=ACT.Tanh, bias=bias1[:, r : r + 1]
                 )
-            lay_out_z(nc.scalar.copy, c, Z_COLS_ON_VECTOR, WIDTH)
 
         def second_layer(c):
             if c < N_CHUNKS:
@@ -182,6 +199,7 @@ def tile_nodelstmcell_pb_t_kernel(tc, h_tilde, k_prev, t0, t1, W1, b1, W2, b2, o
             op0=ALU.mult,
             op1=ALU.add,
         )
+        b2_all = spread(b2_row, "b2_all")
 
         combine_and_turn(1)
         w2_mx = quantise(w2_grouped, const, "w2")
@@ -192,3 +210,5 @@ def tile_nodelstmcell_pb_t_kernel(tc, h_tilde, k_prev, t0, t1, W1, b1, W2, b2, o
                 first_layer(step - 2)
             if step < N_CHUNKS:
                 combine_and_turn(step)
+            if step - 2 < N_CHUNKS:
+                lay_out_z(nc.scalar.copy, step - 2, Z_COLS_ON_VECTOR, WIDTH)

@@ -17,9 +17,9 @@ WIDTH = P * PACK
 BATCH = 4096
 N_CHUNKS = BATCH // WIDTH
 BANK_COLS = 256
-TIME_STEP = 16
 
-Z_COLS_ON_VECTOR = 256
+Z_COLS_ON_VECTOR = 192
+CHUNKS_LAID_OUT_BY_VECTOR = 2
 
 FLOPS = 2 * 2 * BATCH * WIDTH * WIDTH
 
@@ -39,21 +39,17 @@ def tile_nodelstmcell_pb_t_kernel(tc, h_tilde, k_prev, t0, t1, W1, b1, W2, b2, o
         scalar_banks = ctx.enter_context(tc.psum_pool(name="scalar_banks", bufs=4))
         vector_banks = ctx.enter_context(tc.psum_pool(name="vector_banks", bufs=PACK))
 
-        times_row = const.tile([P, 2 * TIME_STEP], BF16)
-        nc.vector.memset(times_row[:], 0.0)
-        nc.scalar.dma_start(out=times_row[0:1, 0:1], in_=t0.rearrange("(o n) -> o n", o=1))
-        nc.scalar.dma_start(
-            out=times_row[0:1, TIME_STEP : TIME_STEP + 1], in_=t1.rearrange("(o n) -> o n", o=1)
-        )
-        b2_row = const.tile([P, WIDTH], BF16)
-        nc.vector.memset(b2_row[:], 0.0)
-        nc.scalar.dma_start(out=b2_row[0:1, :], in_=b2.rearrange("(o n) -> o n", o=1))
+        t0_all = const.tile([P, 1], BF16)
+        t1_all = const.tile([P, 1], BF16)
+        nc.sync.dma_start(out=t0_all[:], in_=t0.partition_broadcast(P))
+        nc.sync.dma_start(out=t1_all[:], in_=t1.partition_broadcast(P))
         b1_rows = const.tile([P, P], BF16)
         nc.vector.memset(b1_rows[:], 0.0)
         nc.scalar.dma_start(out=b1_rows[0:PACK, :], in_=b1.rearrange("(r m) -> r m", m=P))
 
         w1_rows = const.tile([P, PACK, WIDTH + 2], BF16)
         w2_rows = const.tile([P, PACK, WIDTH], BF16)
+        b2_all = const.tile([P, WIDTH], BF16)
         h_rows = []
         k_rows = []
         nc.sync.dma_start(
@@ -66,6 +62,7 @@ def tile_nodelstmcell_pb_t_kernel(tc, h_tilde, k_prev, t0, t1, W1, b1, W2, b2, o
             nc.sync.dma_start(out=k_rows[c][:], in_=k_chunks[c])
             if c == 0:
                 nc.sync.dma_start(out=w2_rows[:], in_=W2.rearrange("(r m) k -> m r k", m=P))
+        nc.sync.dma_start(out=b2_all[:], in_=b2.partition_broadcast(P))
 
         identity = const.tile([P, P], BF16)
         make_identity(nc, identity[:])
@@ -112,25 +109,11 @@ def tile_nodelstmcell_pb_t_kernel(tc, h_tilde, k_prev, t0, t1, W1, b1, W2, b2, o
                 stop=True,
             )
 
-        ones = const.tile([P, P], BF16)
-        nc.vector.memset(ones[:], 1.0)
-
-        def spread(row, name):
-            width = row.shape[1]
-            bank = scalar_banks.tile([P, WIDTH], F32, tag="bank")
-            nc.tensor.matmul(out=bank[:, 0:width], lhsT=ones[:], rhs=row[:], start=True, stop=True)
-            everywhere = const.tile([P, width], F32, name=name)
-            nc.vector.tensor_copy(out=everywhere[:], in_=bank[:, 0:width])
-            return everywhere
-
-        times = spread(times_row, "times")
-        t0_all = times[:, 0:1]
-        t1_all = times[:, TIME_STEP : TIME_STEP + 1]
         half_dt = const.tile([P, 1], F32)
         t_mid = const.tile([P, 1], F32)
-        nc.vector.tensor_sub(out=half_dt[:], in0=t1_all, in1=t0_all)
+        nc.vector.tensor_sub(out=half_dt[:], in0=t1_all[:], in1=t0_all[:])
         nc.vector.tensor_scalar_mul(out=half_dt[:], in0=half_dt[:], scalar1=0.5)
-        nc.vector.tensor_add(out=t_mid[:], in0=t0_all, in1=half_dt[:])
+        nc.vector.tensor_add(out=t_mid[:], in0=t0_all[:], in1=half_dt[:])
 
         y_grouped = {}
         z_planes = {}
@@ -148,6 +131,9 @@ def tile_nodelstmcell_pb_t_kernel(tc, h_tilde, k_prev, t0, t1, W1, b1, W2, b2, o
                 op1=ALU.add,
             )
             y_grouped[c] = turn(y_rows)
+
+        def vector_cols(c):
+            return WIDTH if c < CHUNKS_LAID_OUT_BY_VECTOR else Z_COLS_ON_VECTOR
 
         def lay_out_z(copy, c, first, last):
             copy(
@@ -168,7 +154,7 @@ def tile_nodelstmcell_pb_t_kernel(tc, h_tilde, k_prev, t0, t1, W1, b1, W2, b2, o
 
         def second_layer(c):
             if c < N_CHUNKS:
-                lay_out_z(nc.vector.tensor_copy, c, 0, Z_COLS_ON_VECTOR)
+                lay_out_z(nc.vector.tensor_copy, c, 0, vector_cols(c))
                 sums[c] = []
             if c > 0:
                 result = work.tile([P, PACK, WIDTH], F32)
@@ -199,7 +185,6 @@ def tile_nodelstmcell_pb_t_kernel(tc, h_tilde, k_prev, t0, t1, W1, b1, W2, b2, o
             op0=ALU.mult,
             op1=ALU.add,
         )
-        b2_all = spread(b2_row, "b2_all")
 
         combine_and_turn(1)
         w2_mx = quantise(w2_grouped, const, "w2")
@@ -210,5 +195,5 @@ def tile_nodelstmcell_pb_t_kernel(tc, h_tilde, k_prev, t0, t1, W1, b1, W2, b2, o
                 first_layer(step - 2)
             if step < N_CHUNKS:
                 combine_and_turn(step)
-            if step - 2 < N_CHUNKS:
-                lay_out_z(nc.scalar.copy, step - 2, Z_COLS_ON_VECTOR, WIDTH)
+            if CHUNKS_LAID_OUT_BY_VECTOR <= step - 2 < N_CHUNKS:
+                lay_out_z(nc.scalar.copy, step - 2, vector_cols(step - 2), WIDTH)

@@ -32,7 +32,6 @@ def tile_nodelstmcell_pb_t_kernel(tc, h_tilde, k_prev, t0, t1, W1, b1, W2, b2, o
     out_chunks = out.rearrange("(c q s) n -> c q s n", q=P, s=PACK)
 
     with ExitStack() as ctx:
-        ctx.enter_context(tc.manual_schedule())
         const = ctx.enter_context(tc.tile_pool(name="const", bufs=1))
         inputs = ctx.enter_context(tc.tile_pool(name="inputs", bufs=N_CHUNKS))
         work = ctx.enter_context(tc.tile_pool(name="work", bufs=4))

@@ -17,6 +17,7 @@ WIDTH = P * PACK
 BATCH = 4096
 N_CHUNKS = BATCH // WIDTH
 BANK_COLS = 256
+PAIRS = PACK // 2
 
 Z_COLS_ON_VECTOR = 192
 CHUNKS_LAID_OUT_BY_VECTOR = 2
@@ -42,9 +43,8 @@ def tile_nodelstmcell_pb_t_kernel(tc, h_tilde, k_prev, t0, t1, W1, b1, W2, b2, o
         t1_all = const.tile([P, 1], BF16)
         nc.sync.dma_start(out=t0_all[:], in_=t0.partition_broadcast(P))
         nc.sync.dma_start(out=t1_all[:], in_=t1.partition_broadcast(P))
-        b1_rows = const.tile([P, P], BF16)
-        nc.vector.memset(b1_rows[:], 0.0)
-        nc.scalar.dma_start(out=b1_rows[0:PACK, :], in_=b1.rearrange("(r m) -> r m", m=P))
+        b1_cols = const.tile([P, PACK], BF16)
+        nc.scalar.dma_start(out=b1_cols[:], in_=b1.rearrange("(m t) -> m t", t=PACK))
 
         w1_rows = const.tile([P, PACK, WIDTH + 2], BF16)
         w2_rows = const.tile([P, PACK, WIDTH], BF16)
@@ -52,7 +52,7 @@ def tile_nodelstmcell_pb_t_kernel(tc, h_tilde, k_prev, t0, t1, W1, b1, W2, b2, o
         h_rows = []
         k_rows = []
         nc.sync.dma_start(
-            out=w1_rows[:, :, 0 : WIDTH + 1], in_=W1.rearrange("(r m) k -> m r k", m=P)
+            out=w1_rows[:, :, 0 : WIDTH + 1], in_=W1.rearrange("(m r) k -> m r k", r=PACK)
         )
         for c in range(N_CHUNKS):
             h_rows.append(inputs.tile([P, PACK, WIDTH], BF16, name="h_rows"))
@@ -63,7 +63,7 @@ def tile_nodelstmcell_pb_t_kernel(tc, h_tilde, k_prev, t0, t1, W1, b1, W2, b2, o
                 nc.sync.dma_start(out=w2_rows[:], in_=W2.rearrange("(r m) k -> m r k", m=P))
         nc.sync.dma_start(out=b2_all[:], in_=b2.partition_broadcast(P))
 
-        identity = const.tile([P, P], BF16)
+        identity = const.tile([P, P], F32)
         make_identity(nc, identity[:])
 
         warm = const.tile([P, 1], F32)
@@ -71,19 +71,21 @@ def tile_nodelstmcell_pb_t_kernel(tc, h_tilde, k_prev, t0, t1, W1, b1, W2, b2, o
         nc.scalar.activation(out=warm[:], in_=warm[:], func=ACT.Tanh)
 
         def turn(rows):
+            words = rows[:].bitcast(F32)
             grouped = work.tile([P, WIDTH, PACK], BF16, align_bytes=64)
+            grouped_words = grouped[:].rearrange("p c t -> p (c t)").bitcast(F32)
             for half in range(2):
-                turned = scalar_banks.tile([P, PACK, BANK_COLS], BF16, tag="bank")
+                turned = scalar_banks.tile([P, PAIRS, BANK_COLS], F32, tag="bank")
                 for s in range(2):
-                    for t in range(PACK):
+                    for u in range(PAIRS):
                         nc.tensor.transpose(
-                            turned[:, t, s * P : (s + 1) * P],
-                            rows[:, 2 * half + s, t * P : (t + 1) * P],
+                            turned[:, u, s * P : (s + 1) * P],
+                            words[:, 2 * half + s, u : WIDTH // 2 : PAIRS],
                             identity[:],
                         )
                 nc.scalar.copy(
-                    out=grouped[:, half * BANK_COLS : (half + 1) * BANK_COLS, :],
-                    in_=turned[:].rearrange("p t c -> p c t"),
+                    out=grouped_words[:, half * WIDTH : (half + 1) * WIDTH],
+                    in_=turned[:].rearrange("p u c -> p c u"),
                 )
             return grouped
 
@@ -173,14 +175,12 @@ def tile_nodelstmcell_pb_t_kernel(tc, h_tilde, k_prev, t0, t1, W1, b1, W2, b2, o
         combine_and_turn(0)
         w1_mx = quantise(w1_grouped, const, "w1")
 
-        b1_turned = scalar_banks.tile([P, PACK, BANK_COLS], BF16, tag="bank")
-        nc.tensor.transpose(b1_turned[:, 0, 0:P], b1_rows[:], identity[:])
         bias1 = const.tile([P, PACK], F32)
         nc.vector.scalar_tensor_tensor(
             out=bias1[:],
             in0=w1_rows[:, :, WIDTH],
             scalar=t_mid[:, 0:1],
-            in1=b1_turned[:, 0, 0:PACK],
+            in1=b1_cols[:],
             op0=ALU.mult,
             op1=ALU.add,
         )

@@ -15,12 +15,14 @@ P = 128
 PACK = 4
 WIDTH = P * PACK
 BATCH = 4096
-N_CHUNKS = BATCH // WIDTH
+CHUNK_ROWS = (512,) * 7 + (256, 256)
+N_CHUNKS = len(CHUNK_ROWS)
 BANK_COLS = 256
 PAIRS = PACK // 2
 
-Z_COLS_ON_VECTOR = 192
-CHUNKS_LAID_OUT_BY_VECTOR = 2
+Z_COLS_ON_VECTOR = 128
+CHUNKS_LAID_OUT_BY_VECTOR = 1
+Y_LEAD = 4
 
 FLOPS = 2 * 2 * BATCH * WIDTH * WIDTH
 
@@ -28,9 +30,13 @@ FLOPS = 2 * 2 * BATCH * WIDTH * WIDTH
 def tile_nodelstmcell_pb_t_kernel(tc, h_tilde, k_prev, t0, t1, W1, b1, W2, b2, out):
     nc = tc.nc
 
-    h_chunks = h_tilde.rearrange("(c q s) k -> c q s k", q=P, s=PACK)
-    k_chunks = k_prev.rearrange("(c q s) k -> c q s k", q=P, s=PACK)
-    out_chunks = out.rearrange("(c q s) n -> c q s n", q=P, s=PACK)
+    def chunk_view(x, c):
+        first = sum(CHUNK_ROWS[:c])
+        rows = x[first : first + CHUNK_ROWS[c], :]
+        return rows.rearrange("(q s) k -> q s k", q=P)
+
+    def slots_of(c):
+        return CHUNK_ROWS[c] // P
 
     with ExitStack() as ctx:
         const = ctx.enter_context(tc.tile_pool(name="const", bufs=1))
@@ -51,15 +57,16 @@ def tile_nodelstmcell_pb_t_kernel(tc, h_tilde, k_prev, t0, t1, W1, b1, W2, b2, o
         b2_all = const.tile([P, WIDTH], BF16)
         h_rows = []
         k_rows = []
-        nc.sync.dma_start(
-            out=w1_rows[:, :, 0 : WIDTH + 1], in_=W1.rearrange("(m r) k -> m r k", r=PACK)
-        )
         for c in range(N_CHUNKS):
-            h_rows.append(inputs.tile([P, PACK, WIDTH], BF16, name="h_rows"))
-            k_rows.append(inputs.tile([P, PACK, WIDTH], BF16, name="k_rows"))
-            nc.sync.dma_start(out=h_rows[c][:], in_=h_chunks[c])
-            nc.sync.dma_start(out=k_rows[c][:], in_=k_chunks[c])
+            h_rows.append(inputs.tile([P, slots_of(c), WIDTH], BF16, name="h_rows"))
+            k_rows.append(inputs.tile([P, slots_of(c), WIDTH], BF16, name="k_rows"))
+            nc.sync.dma_start(out=h_rows[c][:], in_=chunk_view(h_tilde, c))
+            nc.sync.dma_start(out=k_rows[c][:], in_=chunk_view(k_prev, c))
             if c == 0:
+                nc.sync.dma_start(
+                    out=w1_rows[:, :, 0 : WIDTH + 1], in_=W1.rearrange("(m r) k -> m r k", r=PACK)
+                )
+            if c == 2:
                 nc.sync.dma_start(out=w2_rows[:], in_=W2.rearrange("(r m) k -> m r k", m=P))
         nc.sync.dma_start(out=b2_all[:], in_=b2.partition_broadcast(P))
 
@@ -70,11 +77,11 @@ def tile_nodelstmcell_pb_t_kernel(tc, h_tilde, k_prev, t0, t1, W1, b1, W2, b2, o
         nc.vector.memset(warm[:], 0.0)
         nc.scalar.activation(out=warm[:], in_=warm[:], func=ACT.Tanh)
 
-        def turn(rows):
+        def turn(rows, slots):
             words = rows[:].bitcast(F32)
-            grouped = work.tile([P, WIDTH, PACK], BF16, align_bytes=64)
+            grouped = work.tile([P, slots * P, PACK], BF16, align_bytes=64)
             grouped_words = grouped[:].rearrange("p c t -> p (c t)").bitcast(F32)
-            for half in range(2):
+            for half in range(slots // 2):
                 turned = scalar_banks.tile([P, PAIRS, BANK_COLS], F32, tag="bank")
                 for s in range(2):
                     for u in range(PAIRS):
@@ -89,9 +96,9 @@ def tile_nodelstmcell_pb_t_kernel(tc, h_tilde, k_prev, t0, t1, W1, b1, W2, b2, o
                 )
             return grouped
 
-        def quantise(grouped, pool, name):
-            codes = pool.tile([P, WIDTH], U32, align_bytes=64, name=name + "_codes")
-            scales = pool.tile([P, WIDTH], U8, align_bytes=64, name=name + "_scales")
+        def quantise(grouped, columns, pool, name):
+            codes = pool.tile([P, columns], U32, align_bytes=64, name=name + "_codes")
+            scales = pool.tile([P, columns], U8, align_bytes=64, name=name + "_scales")
             nc.vector.quantize_mx(
                 out=codes[:].bitcast(FP8X4),
                 scales=scales[:],
@@ -101,7 +108,7 @@ def tile_nodelstmcell_pb_t_kernel(tc, h_tilde, k_prev, t0, t1, W1, b1, W2, b2, o
 
         def multiply(acc, stationary, columns, moving):
             nc.tensor.matmul_mx(
-                out=acc[:],
+                out=acc,
                 lhsT=stationary[0][:, columns].bitcast(FP8X4),
                 lhsT_scale=stationary[1][:, columns],
                 rhs=moving[0][:].bitcast(FP8X4),
@@ -116,25 +123,33 @@ def tile_nodelstmcell_pb_t_kernel(tc, h_tilde, k_prev, t0, t1, W1, b1, W2, b2, o
         nc.vector.tensor_scalar_mul(out=half_dt[:], in0=half_dt[:], scalar1=0.5)
         nc.vector.tensor_add(out=t_mid[:], in0=t0_all[:], in1=half_dt[:])
 
+        y_rows = {}
         y_grouped = {}
+        y_mx = {}
         z_planes = {}
         z_grouped = {}
         sums = {}
 
-        def combine_and_turn(c):
-            y_rows = work.tile([P, PACK, WIDTH], BF16)
+        def combine(c):
+            y_rows[c] = work.tile([P, slots_of(c), WIDTH], BF16, name="y_rows")
             nc.vector.scalar_tensor_tensor(
-                out=y_rows[:],
+                out=y_rows[c][:],
                 in0=k_rows[c][:],
                 scalar=half_dt[:, 0:1],
                 in1=h_rows[c][:],
                 op0=ALU.mult,
                 op1=ALU.add,
             )
-            y_grouped[c] = turn(y_rows)
+
+        def turn_y(c):
+            y_grouped[c] = turn(y_rows[c], slots_of(c))
+
+        def quantise_y(c):
+            y_mx[c] = quantise(y_grouped[c], CHUNK_ROWS[c], work, "y")
 
         def vector_cols(c):
-            return WIDTH if c < CHUNKS_LAID_OUT_BY_VECTOR else Z_COLS_ON_VECTOR
+            last = c >= N_CHUNKS - CHUNKS_LAID_OUT_BY_VECTOR
+            return CHUNK_ROWS[c] if last else Z_COLS_ON_VECTOR
 
         def lay_out_z(copy, c, first, last):
             copy(
@@ -143,38 +158,43 @@ def tile_nodelstmcell_pb_t_kernel(tc, h_tilde, k_prev, t0, t1, W1, b1, W2, b2, o
             )
 
         def first_layer(c):
-            y_mx = quantise(y_grouped[c], work, "y")
-            z_planes[c] = work.tile([P, PACK, WIDTH], BF16, name="z_planes")
-            z_grouped[c] = work.tile([P, WIDTH, PACK], BF16, align_bytes=64, name="z_grouped")
+            rows = CHUNK_ROWS[c]
+            z_planes[c] = work.tile([P, PACK, rows], BF16, name="z_planes")
+            z_grouped[c] = work.tile([P, rows, PACK], BF16, align_bytes=64, name="z_grouped")
             for r in range(PACK):
-                hidden = scalar_banks.tile([P, WIDTH], F32, tag="bank")
-                multiply(hidden, w1_mx, slice(r * P, (r + 1) * P), y_mx)
+                hidden = scalar_banks.tile([P, rows], F32, tag="bank")
+                multiply(hidden[:], w1_mx, slice(r * P, (r + 1) * P), y_mx[c])
                 nc.scalar.activation(
                     out=z_planes[c][:, r, :], in_=hidden[:], func=ACT.Tanh, bias=bias1[:, r : r + 1]
                 )
 
         def second_layer(c):
-            if c < N_CHUNKS:
-                lay_out_z(nc.vector.tensor_copy, c, 0, vector_cols(c))
-                sums[c] = []
-            if c > 0:
-                result = work.tile([P, PACK, WIDTH], F32)
-            for s in range(PACK):
-                if c > 0:
+            def finish(s):
+                if c > 0 and s < slots_of(c - 1):
                     nc.vector.tensor_add(out=result[:, s, :], in0=sums[c - 1][s][:], in1=b2_all[:])
-                    nc.sync.dma_start(out=out_chunks[c - 1][:, s, :], in_=result[:, s, :])
-                if c < N_CHUNKS:
-                    if s == 0:
-                        z_mx = quantise(z_grouped[c], work, "z")
+                    nc.sync.dma_start(out=chunk_view(out, c - 1)[:, s, :], in_=result[:, s, :])
+
+            if c > 0:
+                result = work.tile([P, slots_of(c - 1), WIDTH], F32)
+            if c < N_CHUNKS:
+                if vector_cols(c) > 0:
+                    lay_out_z(nc.vector.tensor_copy, c, 0, vector_cols(c))
+                sums[c] = []
+            finish(0)
+            if c < N_CHUNKS:
+                z_mx = quantise(z_grouped[c], CHUNK_ROWS[c], work, "z")
+            for s in range(PACK):
+                finish(s + 1)
+                if c < N_CHUNKS and s < slots_of(c):
                     summed = vector_banks.tile([P, WIDTH], F32)
-                    multiply(summed, z_mx, slice(s * P, (s + 1) * P), w2_mx)
+                    multiply(summed[:], z_mx, slice(s * P, (s + 1) * P), w2_mx)
                     sums[c].append(summed)
 
-        w1_grouped = turn(w1_rows)
-        w2_grouped = turn(w2_rows)
-        combine_and_turn(0)
-        w1_mx = quantise(w1_grouped, const, "w1")
-
+        ctx.enter_context(tc.manual_schedule())
+        combine(0)
+        w1_grouped = turn(w1_rows, PACK)
+        turn_y(0)
+        w1_mx = quantise(w1_grouped, WIDTH, const, "w1")
         bias1 = const.tile([P, PACK], F32)
         nc.vector.scalar_tensor_tensor(
             out=bias1[:],
@@ -185,14 +205,27 @@ def tile_nodelstmcell_pb_t_kernel(tc, h_tilde, k_prev, t0, t1, W1, b1, W2, b2, o
             op1=ALU.add,
         )
 
-        combine_and_turn(1)
-        w2_mx = quantise(w2_grouped, const, "w2")
-        for step in range(2, N_CHUNKS + 5):
-            if step >= 4:
-                second_layer(step - 4)
-            if step - 2 < N_CHUNKS:
-                first_layer(step - 2)
-            if step < N_CHUNKS:
-                combine_and_turn(step)
-            if CHUNKS_LAID_OUT_BY_VECTOR <= step - 2 < N_CHUNKS:
-                lay_out_z(nc.scalar.copy, step - 2, vector_cols(step - 2), WIDTH)
+        quantise_y(0)
+        first_layer(0)
+        combine(1)
+        turn_y(1)
+        for c in range(2, Y_LEAD):
+            combine(c)
+        for c in range(N_CHUNKS + 2):
+            if 0 < c < N_CHUNKS:
+                first_layer(c)
+            if 0 < c and c + 2 < N_CHUNKS:
+                turn_y(c + 2)
+            if c == 0:
+                turn_y(2)
+                w2_grouped = turn(w2_rows, PACK)
+            if c + 1 < N_CHUNKS:
+                quantise_y(c + 1)
+            if c == 0:
+                w2_mx = quantise(w2_grouped, WIDTH, const, "w2")
+            if 1 <= c:
+                second_layer(c - 1)
+            if c + Y_LEAD < N_CHUNKS:
+                combine(c + Y_LEAD)
+            if c < N_CHUNKS - CHUNKS_LAID_OUT_BY_VECTOR:
+                lay_out_z(nc.scalar.copy, c, vector_cols(c), CHUNK_ROWS[c])

@@ -15,13 +15,14 @@ P = 128
 PACK = 4
 WIDTH = P * PACK
 BATCH = 4096
-CHUNK_ROWS = (512,) * 7 + (256, 256)
+CHUNK_ROWS = (256,) + (512,) * 7 + (256,)
 N_CHUNKS = len(CHUNK_ROWS)
-BANK_COLS = 256
+SLOTS_IN_BANK = 2
 PAIRS = PACK // 2
 
-Z_COLS_ON_VECTOR = 128
+Z_PART_ON_VECTOR = 1 / 2
 CHUNKS_LAID_OUT_BY_VECTOR = 1
+CHUNKS_SHARED_WITH_TENSOR_ENGINE = 8
 Y_LEAD = 4
 
 FLOPS = 2 * 2 * BATCH * WIDTH * WIDTH
@@ -37,6 +38,9 @@ def tile_nodelstmcell_pb_t_kernel(tc, h_tilde, k_prev, t0, t1, W1, b1, W2, b2, o
 
     def slots_of(c):
         return CHUNK_ROWS[c] // P
+
+    def vector_slots(c):
+        return slots_of(c) - (c < CHUNKS_SHARED_WITH_TENSOR_ENGINE)
 
     with ExitStack() as ctx:
         const = ctx.enter_context(tc.tile_pool(name="const", bufs=1))
@@ -57,44 +61,71 @@ def tile_nodelstmcell_pb_t_kernel(tc, h_tilde, k_prev, t0, t1, W1, b1, W2, b2, o
         b2_all = const.tile([P, WIDTH], BF16)
         h_rows = []
         k_rows = []
+        nc.sync.dma_start(
+            out=w1_rows[:, :, 0 : WIDTH + 1], in_=W1.rearrange("(m r) k -> m r k", r=PACK)
+        )
         for c in range(N_CHUNKS):
             h_rows.append(inputs.tile([P, slots_of(c), WIDTH], BF16, name="h_rows"))
             k_rows.append(inputs.tile([P, slots_of(c), WIDTH], BF16, name="k_rows"))
             nc.sync.dma_start(out=h_rows[c][:], in_=chunk_view(h_tilde, c))
             nc.sync.dma_start(out=k_rows[c][:], in_=chunk_view(k_prev, c))
-            if c == 0:
-                nc.sync.dma_start(
-                    out=w1_rows[:, :, 0 : WIDTH + 1], in_=W1.rearrange("(m r) k -> m r k", r=PACK)
-                )
-            if c == 2:
+            if c == 1:
                 nc.sync.dma_start(out=w2_rows[:], in_=W2.rearrange("(r m) k -> m r k", m=P))
         nc.sync.dma_start(out=b2_all[:], in_=b2.partition_broadcast(P))
 
         identity = const.tile([P, P], F32)
         make_identity(nc, identity[:])
+        turn_h = const.tile([P, P], BF16)
+        turn_k1 = const.tile([P, P], BF16)
+        turn_k0 = const.tile([P, P], BF16)
+        nc.vector.tensor_copy(out=turn_h[:], in_=identity[:])
 
         warm = const.tile([P, 1], F32)
         nc.vector.memset(warm[:], 0.0)
         nc.scalar.activation(out=warm[:], in_=warm[:], func=ACT.Tanh)
 
-        def turn(rows, slots):
+        def turn(rows, slots, grouped, word_index):
             words = rows[:].bitcast(F32)
-            grouped = work.tile([P, slots * P, PACK], BF16, align_bytes=64)
             grouped_words = grouped[:].rearrange("p c t -> p (c t)").bitcast(F32)
-            for half in range(slots // 2):
-                turned = scalar_banks.tile([P, PAIRS, BANK_COLS], F32, tag="bank")
-                for s in range(2):
+            for first in range(0, slots, SLOTS_IN_BANK):
+                n = min(SLOTS_IN_BANK, slots - first)
+                turned = scalar_banks.tile([P, PAIRS, n * P], F32, tag="bank")
+                for s in range(n):
                     for u in range(PAIRS):
                         nc.tensor.transpose(
                             turned[:, u, s * P : (s + 1) * P],
-                            words[:, 2 * half + s, u : WIDTH // 2 : PAIRS],
+                            words[:, first + s, word_index(u)],
                             identity[:],
                         )
                 nc.scalar.copy(
-                    out=grouped_words[:, half * WIDTH : (half + 1) * WIDTH],
+                    out=grouped_words[:, first * P * PAIRS : (first + n) * P * PAIRS],
                     in_=turned[:].rearrange("p u c -> p c u"),
                 )
-            return grouped
+
+        def halves(u):
+            return slice(u * P, (u + 1) * P)
+
+        def alternate(u):
+            return slice(u, WIDTH // 2, PAIRS)
+
+        def combine_on_tensor_engine(c, s):
+            turned = scalar_banks.tile([P, PACK, P], F32, tag="bank")
+            for t in range(PACK):
+                u, e = divmod(t, 2)
+                values = slice(2 * P * u + e, 2 * P * (u + 1), 2)
+                terms = ((h_rows[c], turn_h), (k_rows[c], turn_k1), (k_rows[c], turn_k0))
+                for i, (rows, moving) in enumerate(terms):
+                    nc.tensor.matmul(
+                        turned[:, t, :],
+                        lhsT=rows[:, s, values],
+                        rhs=moving[:],
+                        start=i == 0,
+                        stop=i == len(terms) - 1,
+                    )
+            nc.scalar.copy(
+                out=y_grouped[c][:, s * P : (s + 1) * P, :],
+                in_=turned[:].rearrange("p t c -> p c t"),
+            )
 
         def quantise(grouped, columns, pool, name):
             codes = pool.tile([P, columns], U32, align_bytes=64, name=name + "_codes")
@@ -117,10 +148,15 @@ def tile_nodelstmcell_pb_t_kernel(tc, h_tilde, k_prev, t0, t1, W1, b1, W2, b2, o
                 stop=True,
             )
 
+        half_t1 = const.tile([P, 1], F32)
+        minus_half_t0 = const.tile([P, 1], F32)
         half_dt = const.tile([P, 1], F32)
         t_mid = const.tile([P, 1], F32)
-        nc.vector.tensor_sub(out=half_dt[:], in0=t1_all[:], in1=t0_all[:])
-        nc.vector.tensor_scalar_mul(out=half_dt[:], in0=half_dt[:], scalar1=0.5)
+        nc.vector.tensor_scalar_mul(out=half_t1[:], in0=t1_all[:], scalar1=0.5)
+        nc.vector.tensor_scalar_mul(out=minus_half_t0[:], in0=t0_all[:], scalar1=-0.5)
+        nc.vector.tensor_add(out=half_dt[:], in0=half_t1[:], in1=minus_half_t0[:])
+        nc.vector.tensor_scalar_mul(out=turn_k1[:], in0=turn_h[:], scalar1=half_t1[:, 0:1])
+        nc.vector.tensor_scalar_mul(out=turn_k0[:], in0=turn_h[:], scalar1=minus_half_t0[:, 0:1])
         nc.vector.tensor_add(out=t_mid[:], in0=t0_all[:], in1=half_dt[:])
 
         y_rows = {}
@@ -131,25 +167,31 @@ def tile_nodelstmcell_pb_t_kernel(tc, h_tilde, k_prev, t0, t1, W1, b1, W2, b2, o
         sums = {}
 
         def combine(c):
-            y_rows[c] = work.tile([P, slots_of(c), WIDTH], BF16, name="y_rows")
+            n = vector_slots(c)
+            y_rows[c] = work.tile([P, n, WIDTH], BF16, name="y_rows")
             nc.vector.scalar_tensor_tensor(
                 out=y_rows[c][:],
-                in0=k_rows[c][:],
+                in0=k_rows[c][:, 0:n, :],
                 scalar=half_dt[:, 0:1],
-                in1=h_rows[c][:],
+                in1=h_rows[c][:, 0:n, :],
                 op0=ALU.mult,
                 op1=ALU.add,
             )
 
         def turn_y(c):
-            y_grouped[c] = turn(y_rows[c], slots_of(c))
+            y_grouped[c] = work.tile(
+                [P, CHUNK_ROWS[c], PACK], BF16, align_bytes=64, name="y_grouped"
+            )
+            for s in range(vector_slots(c), slots_of(c)):
+                combine_on_tensor_engine(c, s)
+            turn(y_rows[c], vector_slots(c), y_grouped[c], halves)
 
         def quantise_y(c):
             y_mx[c] = quantise(y_grouped[c], CHUNK_ROWS[c], work, "y")
 
         def vector_cols(c):
             last = c >= N_CHUNKS - CHUNKS_LAID_OUT_BY_VECTOR
-            return CHUNK_ROWS[c] if last else Z_COLS_ON_VECTOR
+            return CHUNK_ROWS[c] if last else int(CHUNK_ROWS[c] * Z_PART_ON_VECTOR)
 
         def lay_out_z(copy, c, first, last):
             copy(
@@ -181,10 +223,11 @@ def tile_nodelstmcell_pb_t_kernel(tc, h_tilde, k_prev, t0, t1, W1, b1, W2, b2, o
                     lay_out_z(nc.vector.tensor_copy, c, 0, vector_cols(c))
                 sums[c] = []
             finish(0)
+            finish(1)
             if c < N_CHUNKS:
                 z_mx = quantise(z_grouped[c], CHUNK_ROWS[c], work, "z")
             for s in range(PACK):
-                finish(s + 1)
+                finish(s + 2)
                 if c < N_CHUNKS and s < slots_of(c):
                     summed = vector_banks.tile([P, WIDTH], F32)
                     multiply(summed[:], z_mx, slice(s * P, (s + 1) * P), w2_mx)
@@ -192,7 +235,8 @@ def tile_nodelstmcell_pb_t_kernel(tc, h_tilde, k_prev, t0, t1, W1, b1, W2, b2, o
 
         ctx.enter_context(tc.manual_schedule())
         combine(0)
-        w1_grouped = turn(w1_rows, PACK)
+        w1_grouped = const.tile([P, WIDTH, PACK], BF16, align_bytes=64)
+        turn(w1_rows, PACK, w1_grouped, halves)
         turn_y(0)
         w1_mx = quantise(w1_grouped, WIDTH, const, "w1")
         bias1 = const.tile([P, PACK], F32)
@@ -205,6 +249,7 @@ def tile_nodelstmcell_pb_t_kernel(tc, h_tilde, k_prev, t0, t1, W1, b1, W2, b2, o
             op1=ALU.add,
         )
 
+        w2_grouped = const.tile([P, WIDTH, PACK], BF16, align_bytes=64)
         quantise_y(0)
         first_layer(0)
         combine(1)
@@ -218,7 +263,7 @@ def tile_nodelstmcell_pb_t_kernel(tc, h_tilde, k_prev, t0, t1, W1, b1, W2, b2, o
                 turn_y(c + 2)
             if c == 0:
                 turn_y(2)
-                w2_grouped = turn(w2_rows, PACK)
+                turn(w2_rows, PACK, w2_grouped, alternate)
             if c + 1 < N_CHUNKS:
                 quantise_y(c + 1)
             if c == 0:

@@ -98,8 +98,10 @@ def tile_nodelstmcell_pb_t_kernel(tc, h_tilde, k_prev, t0, t1, W1, b1, W2, b2, o
                             identity[:],
                         )
                 nc.scalar.copy(
-                    out=grouped_words[:, first * P * PAIRS : (first + n) * P * PAIRS],
-                    in_=turned[:].rearrange("p u c -> p c u"),
+                    out=grouped_words[:, first * P * PAIRS : (first + n) * P * PAIRS].rearrange(
+                        "p (c i u) -> p c u i", i=2, u=PAIRS
+                    ),
+                    in_=turned[:].rearrange("p u (c i) -> p c u i", i=2),
                 )
 
         def halves(u):
@@ -123,8 +125,10 @@ def tile_nodelstmcell_pb_t_kernel(tc, h_tilde, k_prev, t0, t1, W1, b1, W2, b2, o
                         stop=i == len(terms) - 1,
                     )
             nc.scalar.copy(
-                out=y_grouped[c][:, s * P : (s + 1) * P, :],
-                in_=turned[:].rearrange("p t c -> p c t"),
+                out=y_grouped[c][:, s * P : (s + 1) * P, :].rearrange(
+                    "p (c i) t -> p c t i", i=2
+                ),
+                in_=turned[:].rearrange("p t (c i) -> p c t i", i=2),
             )
 
         def quantise(grouped, columns, pool, name):

@@ -15,15 +15,14 @@ P = 128
 PACK = 4
 WIDTH = P * PACK
 BATCH = 4096
-CHUNK_ROWS = (256,) + (512,) * 7 + (256,)
+CHUNK_ROWS = (512,) * 7 + (256, 256)
 N_CHUNKS = len(CHUNK_ROWS)
 SLOTS_IN_BANK = 2
 PAIRS = PACK // 2
 
-Z_PART_ON_VECTOR = 1 / 2
-CHUNKS_LAID_OUT_BY_VECTOR = 1
-CHUNKS_SHARED_WITH_TENSOR_ENGINE = 8
-Y_LEAD = 4
+Z_PART_ON_VECTOR = (1 / 2,) * 4 + (1 / 4,) * 4 + (1,)
+VECTOR_BANKS = 4
+Y_LEAD = 5
 
 FLOPS = 2 * 2 * BATCH * WIDTH * WIDTH
 
@@ -39,15 +38,12 @@ def tile_nodelstmcell_pb_t_kernel(tc, h_tilde, k_prev, t0, t1, W1, b1, W2, b2, o
     def slots_of(c):
         return CHUNK_ROWS[c] // P
 
-    def vector_slots(c):
-        return slots_of(c) - (c < CHUNKS_SHARED_WITH_TENSOR_ENGINE)
-
     with ExitStack() as ctx:
         const = ctx.enter_context(tc.tile_pool(name="const", bufs=1))
         inputs = ctx.enter_context(tc.tile_pool(name="inputs", bufs=N_CHUNKS))
         work = ctx.enter_context(tc.tile_pool(name="work", bufs=4))
         scalar_banks = ctx.enter_context(tc.psum_pool(name="scalar_banks", bufs=4))
-        vector_banks = ctx.enter_context(tc.psum_pool(name="vector_banks", bufs=PACK))
+        vector_banks = ctx.enter_context(tc.psum_pool(name="vector_banks", bufs=VECTOR_BANKS))
 
         t0_all = const.tile([P, 1], BF16)
         t1_all = const.tile([P, 1], BF16)
@@ -75,10 +71,6 @@ def tile_nodelstmcell_pb_t_kernel(tc, h_tilde, k_prev, t0, t1, W1, b1, W2, b2, o
 
         identity = const.tile([P, P], F32)
         make_identity(nc, identity[:])
-        turn_h = const.tile([P, P], BF16)
-        turn_k1 = const.tile([P, P], BF16)
-        turn_k0 = const.tile([P, P], BF16)
-        nc.vector.tensor_copy(out=turn_h[:], in_=identity[:])
 
         warm = const.tile([P, 1], F32)
         nc.vector.memset(warm[:], 0.0)
@@ -110,27 +102,6 @@ def tile_nodelstmcell_pb_t_kernel(tc, h_tilde, k_prev, t0, t1, W1, b1, W2, b2, o
         def alternate(u):
             return slice(u, WIDTH // 2, PAIRS)
 
-        def combine_on_tensor_engine(c, s):
-            turned = scalar_banks.tile([P, PACK, P], F32, tag="bank")
-            for t in range(PACK):
-                u, e = divmod(t, 2)
-                values = slice(2 * P * u + e, 2 * P * (u + 1), 2)
-                terms = ((h_rows[c], turn_h), (k_rows[c], turn_k1), (k_rows[c], turn_k0))
-                for i, (rows, moving) in enumerate(terms):
-                    nc.tensor.matmul(
-                        turned[:, t, :],
-                        lhsT=rows[:, s, values],
-                        rhs=moving[:],
-                        start=i == 0,
-                        stop=i == len(terms) - 1,
-                    )
-            nc.scalar.copy(
-                out=y_grouped[c][:, s * P : (s + 1) * P, :].rearrange(
-                    "p (c i) t -> p c t i", i=2
-                ),
-                in_=turned[:].rearrange("p t (c i) -> p c t i", i=2),
-            )
-
         def quantise(grouped, columns, pool, name):
             codes = pool.tile([P, columns], U32, align_bytes=64, name=name + "_codes")
             scales = pool.tile([P, columns], U8, align_bytes=64, name=name + "_scales")
@@ -152,15 +123,10 @@ def tile_nodelstmcell_pb_t_kernel(tc, h_tilde, k_prev, t0, t1, W1, b1, W2, b2, o
                 stop=True,
             )
 
-        half_t1 = const.tile([P, 1], F32)
-        minus_half_t0 = const.tile([P, 1], F32)
         half_dt = const.tile([P, 1], F32)
         t_mid = const.tile([P, 1], F32)
-        nc.vector.tensor_scalar_mul(out=half_t1[:], in0=t1_all[:], scalar1=0.5)
-        nc.vector.tensor_scalar_mul(out=minus_half_t0[:], in0=t0_all[:], scalar1=-0.5)
-        nc.vector.tensor_add(out=half_dt[:], in0=half_t1[:], in1=minus_half_t0[:])
-        nc.vector.tensor_scalar_mul(out=turn_k1[:], in0=turn_h[:], scalar1=half_t1[:, 0:1])
-        nc.vector.tensor_scalar_mul(out=turn_k0[:], in0=turn_h[:], scalar1=minus_half_t0[:, 0:1])
+        nc.vector.tensor_sub(out=half_dt[:], in0=t1_all[:], in1=t0_all[:])
+        nc.vector.tensor_scalar_mul(out=half_dt[:], in0=half_dt[:], scalar1=0.5)
         nc.vector.tensor_add(out=t_mid[:], in0=t0_all[:], in1=half_dt[:])
 
         y_rows = {}
@@ -168,16 +134,17 @@ def tile_nodelstmcell_pb_t_kernel(tc, h_tilde, k_prev, t0, t1, W1, b1, W2, b2, o
         y_mx = {}
         z_planes = {}
         z_grouped = {}
-        sums = {}
+        hidden = {}
+        result = {}
+        waiting = []
 
         def combine(c):
-            n = vector_slots(c)
-            y_rows[c] = work.tile([P, n, WIDTH], BF16, name="y_rows")
+            y_rows[c] = work.tile([P, slots_of(c), WIDTH], BF16, name="y_rows")
             nc.vector.scalar_tensor_tensor(
                 out=y_rows[c][:],
-                in0=k_rows[c][:, 0:n, :],
+                in0=k_rows[c][:],
                 scalar=half_dt[:, 0:1],
-                in1=h_rows[c][:, 0:n, :],
+                in1=h_rows[c][:],
                 op0=ALU.mult,
                 op1=ALU.add,
             )
@@ -186,16 +153,13 @@ def tile_nodelstmcell_pb_t_kernel(tc, h_tilde, k_prev, t0, t1, W1, b1, W2, b2, o
             y_grouped[c] = work.tile(
                 [P, CHUNK_ROWS[c], PACK], BF16, align_bytes=64, name="y_grouped"
             )
-            for s in range(vector_slots(c), slots_of(c)):
-                combine_on_tensor_engine(c, s)
-            turn(y_rows[c], vector_slots(c), y_grouped[c], halves)
+            turn(y_rows[c], slots_of(c), y_grouped[c], halves)
 
         def quantise_y(c):
             y_mx[c] = quantise(y_grouped[c], CHUNK_ROWS[c], work, "y")
 
         def vector_cols(c):
-            last = c >= N_CHUNKS - CHUNKS_LAID_OUT_BY_VECTOR
-            return CHUNK_ROWS[c] if last else int(CHUNK_ROWS[c] * Z_PART_ON_VECTOR)
+            return int(CHUNK_ROWS[c] * Z_PART_ON_VECTOR[c])
 
         def lay_out_z(copy, c, first, last):
             copy(
@@ -203,45 +167,52 @@ def tile_nodelstmcell_pb_t_kernel(tc, h_tilde, k_prev, t0, t1, W1, b1, W2, b2, o
                 in_=z_planes[c][:, :, first:last].rearrange("p t (c i) -> p c t i", i=4),
             )
 
-        def first_layer(c):
+        def hidden_sums(c):
+            hidden[c] = []
+            for r in range(PACK):
+                bank = scalar_banks.tile([P, CHUNK_ROWS[c]], F32, tag="bank")
+                multiply(bank[:], w1_mx, slice(r * P, (r + 1) * P), y_mx[c])
+                hidden[c].append(bank)
+
+        def hidden_tanh(c):
             rows = CHUNK_ROWS[c]
             z_planes[c] = work.tile([P, PACK, rows], BF16, name="z_planes")
             z_grouped[c] = work.tile([P, rows, PACK], BF16, align_bytes=64, name="z_grouped")
             for r in range(PACK):
-                hidden = scalar_banks.tile([P, rows], F32, tag="bank")
-                multiply(hidden[:], w1_mx, slice(r * P, (r + 1) * P), y_mx[c])
                 nc.scalar.activation(
-                    out=z_planes[c][:, r, :], in_=hidden[:], func=ACT.Tanh, bias=bias1[:, r : r + 1]
+                    out=z_planes[c][:, r, :],
+                    in_=hidden[c][r][:],
+                    func=ACT.Tanh,
+                    bias=bias1[:, r : r + 1],
                 )
 
-        def second_layer(c):
-            def finish(s):
-                if c > 0 and s < slots_of(c - 1):
-                    nc.vector.tensor_add(out=result[:, s, :], in0=sums[c - 1][s][:], in1=b2_all[:])
-                    nc.sync.dma_start(out=chunk_view(out, c - 1)[:, s, :], in_=result[:, s, :])
+        def finish_oldest_sum():
+            c, s, summed = waiting[0]
+            waiting[:] = waiting[1:]
+            nc.vector.tensor_add(out=result[c][:, s, :], in0=summed[:], in1=b2_all[:])
+            nc.sync.dma_start(out=chunk_view(out, c)[:, s, :], in_=result[c][:, s, :])
 
-            if c > 0:
-                result = work.tile([P, slots_of(c - 1), WIDTH], F32)
-            if c < N_CHUNKS:
-                if vector_cols(c) > 0:
-                    lay_out_z(nc.vector.tensor_copy, c, 0, vector_cols(c))
-                sums[c] = []
-            finish(0)
-            finish(1)
-            if c < N_CHUNKS:
-                z_mx = quantise(z_grouped[c], CHUNK_ROWS[c], work, "z")
-            for s in range(PACK):
-                finish(s + 2)
-                if c < N_CHUNKS and s < slots_of(c):
-                    summed = vector_banks.tile([P, WIDTH], F32)
-                    multiply(summed[:], z_mx, slice(s * P, (s + 1) * P), w2_mx)
-                    sums[c].append(summed)
+        def second_layer(c):
+            if vector_cols(c) > 0:
+                lay_out_z(nc.vector.tensor_copy, c, 0, vector_cols(c))
+            for _ in range(min(2, len(waiting))):
+                finish_oldest_sum()
+            z_mx = quantise(z_grouped[c], CHUNK_ROWS[c], work, "z")
+            result[c] = work.tile([P, slots_of(c), WIDTH], F32, name="result")
+            for s in range(slots_of(c)):
+                if len(waiting) == VECTOR_BANKS:
+                    finish_oldest_sum()
+                summed = vector_banks.tile([P, WIDTH], F32)
+                multiply(summed[:], z_mx, slice(s * P, (s + 1) * P), w2_mx)
+                waiting.append((c, s, summed))
 
         ctx.enter_context(tc.manual_schedule())
         combine(0)
         w1_grouped = const.tile([P, WIDTH, PACK], BF16, align_bytes=64)
         turn(w1_rows, PACK, w1_grouped, halves)
         turn_y(0)
+        combine(1)
+        turn_y(1)
         w1_mx = quantise(w1_grouped, WIDTH, const, "w1")
         bias1 = const.tile([P, PACK], F32)
         nc.vector.scalar_tensor_tensor(
@@ -255,26 +226,27 @@ def tile_nodelstmcell_pb_t_kernel(tc, h_tilde, k_prev, t0, t1, W1, b1, W2, b2, o
 
         w2_grouped = const.tile([P, WIDTH, PACK], BF16, align_bytes=64)
         quantise_y(0)
-        first_layer(0)
-        combine(1)
-        turn_y(1)
+        hidden_sums(0)
         for c in range(2, Y_LEAD):
             combine(c)
-        for c in range(N_CHUNKS + 2):
-            if 0 < c < N_CHUNKS:
-                first_layer(c)
-            if 0 < c and c + 2 < N_CHUNKS:
+        for c in range(N_CHUNKS + 1):
+            if c < N_CHUNKS:
+                hidden_tanh(c)
+            if c + 2 < N_CHUNKS:
                 turn_y(c + 2)
             if c == 0:
-                turn_y(2)
                 turn(w2_rows, PACK, w2_grouped, alternate)
             if c + 1 < N_CHUNKS:
                 quantise_y(c + 1)
             if c == 0:
                 w2_mx = quantise(w2_grouped, WIDTH, const, "w2")
-            if 1 <= c:
+            if c + 1 < N_CHUNKS:
+                hidden_sums(c + 1)
+            if c >= 1:
                 second_layer(c - 1)
             if c + Y_LEAD < N_CHUNKS:
                 combine(c + Y_LEAD)
-            if c < N_CHUNKS - CHUNKS_LAID_OUT_BY_VECTOR:
+            if c < N_CHUNKS and vector_cols(c) < CHUNK_ROWS[c]:
                 lay_out_z(nc.scalar.copy, c, vector_cols(c), CHUNK_ROWS[c])
+        while waiting:
+            finish_oldest_sum()

@@ -20,9 +20,11 @@ N_CHUNKS = len(CHUNK_ROWS)
 SLOTS_IN_BANK = 2
 PAIRS = PACK // 2
 
-Z_PART_ON_VECTOR = (1 / 2,) * 4 + (1 / 4,) * 4 + (1,)
+Z_PART_ON_VECTOR = (1 / 4,) * 4 + (3 / 8,) * 4 + (1,)
+TIME_GAP = 16
 VECTOR_BANKS = 4
-Y_LEAD = 5
+Y_LEAD = 4
+CHUNKS_IN_HALVES = 2
 
 FLOPS = 2 * 2 * BATCH * WIDTH * WIDTH
 
@@ -38,6 +40,11 @@ def tile_nodelstmcell_pb_t_kernel(tc, h_tilde, k_prev, t0, t1, W1, b1, W2, b2, o
     def slots_of(c):
         return CHUNK_ROWS[c] // P
 
+    def parts_of(c):
+        slots = slots_of(c)
+        step = slots // 2 if c < CHUNKS_IN_HALVES else slots
+        return [slice(s, s + step) for s in range(0, slots, step)]
+
     with ExitStack() as ctx:
         const = ctx.enter_context(tc.tile_pool(name="const", bufs=1))
         inputs = ctx.enter_context(tc.tile_pool(name="inputs", bufs=N_CHUNKS))
@@ -45,16 +52,25 @@ def tile_nodelstmcell_pb_t_kernel(tc, h_tilde, k_prev, t0, t1, W1, b1, W2, b2, o
         scalar_banks = ctx.enter_context(tc.psum_pool(name="scalar_banks", bufs=4))
         vector_banks = ctx.enter_context(tc.psum_pool(name="vector_banks", bufs=VECTOR_BANKS))
 
-        t0_all = const.tile([P, 1], BF16)
-        t1_all = const.tile([P, 1], BF16)
-        nc.sync.dma_start(out=t0_all[:], in_=t0.partition_broadcast(P))
-        nc.sync.dma_start(out=t1_all[:], in_=t1.partition_broadcast(P))
+        times = const.tile([P, 2 * TIME_GAP], BF16)
+        halves_signed = const.tile([P, P], BF16)
+        ones = const.tile([P, P], BF16)
+        b2_row = const.tile([P, WIDTH], BF16)
+        nc.vector.memset(times[:], 0.0)
+        nc.vector.memset(halves_signed[:], 0.5)
+        nc.vector.memset(halves_signed[32:64, :], -0.5)
+        nc.vector.memset(b2_row[:], 0.0)
+        nc.vector.memset(ones[:], 1.0)
+        for time, row, col in ((t1, 0, 0), (t0, 32, 0), (t1, 0, TIME_GAP), (t0, 64, TIME_GAP)):
+            nc.scalar.dma_start(
+                out=times[row : row + 1, col : col + 1], in_=time.rearrange("(o n) -> o n", o=1)
+            )
         b1_cols = const.tile([P, PACK], BF16)
         nc.scalar.dma_start(out=b1_cols[:], in_=b1.rearrange("(m t) -> m t", t=PACK))
+        nc.scalar.dma_start(out=b2_row[0:1, :], in_=b2.rearrange("(o n) -> o n", o=1))
 
         w1_rows = const.tile([P, PACK, WIDTH + 2], BF16)
         w2_rows = const.tile([P, PACK, WIDTH], BF16)
-        b2_all = const.tile([P, WIDTH], BF16)
         h_rows = []
         k_rows = []
         nc.sync.dma_start(
@@ -63,11 +79,11 @@ def tile_nodelstmcell_pb_t_kernel(tc, h_tilde, k_prev, t0, t1, W1, b1, W2, b2, o
         for c in range(N_CHUNKS):
             h_rows.append(inputs.tile([P, slots_of(c), WIDTH], BF16, name="h_rows"))
             k_rows.append(inputs.tile([P, slots_of(c), WIDTH], BF16, name="k_rows"))
-            nc.sync.dma_start(out=h_rows[c][:], in_=chunk_view(h_tilde, c))
-            nc.sync.dma_start(out=k_rows[c][:], in_=chunk_view(k_prev, c))
-            if c == 1:
+            for part in parts_of(c):
+                nc.sync.dma_start(out=h_rows[c][:, part, :], in_=chunk_view(h_tilde, c)[:, part, :])
+                nc.sync.dma_start(out=k_rows[c][:, part, :], in_=chunk_view(k_prev, c)[:, part, :])
+            if c == 2:
                 nc.sync.dma_start(out=w2_rows[:], in_=W2.rearrange("(r m) k -> m r k", m=P))
-        nc.sync.dma_start(out=b2_all[:], in_=b2.partition_broadcast(P))
 
         identity = const.tile([P, P], F32)
         make_identity(nc, identity[:])
@@ -123,12 +139,6 @@ def tile_nodelstmcell_pb_t_kernel(tc, h_tilde, k_prev, t0, t1, W1, b1, W2, b2, o
                 stop=True,
             )
 
-        half_dt = const.tile([P, 1], F32)
-        t_mid = const.tile([P, 1], F32)
-        nc.vector.tensor_sub(out=half_dt[:], in0=t1_all[:], in1=t0_all[:])
-        nc.vector.tensor_scalar_mul(out=half_dt[:], in0=half_dt[:], scalar1=0.5)
-        nc.vector.tensor_add(out=t_mid[:], in0=t0_all[:], in1=half_dt[:])
-
         y_rows = {}
         y_grouped = {}
         y_mx = {}
@@ -140,14 +150,15 @@ def tile_nodelstmcell_pb_t_kernel(tc, h_tilde, k_prev, t0, t1, W1, b1, W2, b2, o
 
         def combine(c):
             y_rows[c] = work.tile([P, slots_of(c), WIDTH], BF16, name="y_rows")
-            nc.vector.scalar_tensor_tensor(
-                out=y_rows[c][:],
-                in0=k_rows[c][:],
-                scalar=half_dt[:, 0:1],
-                in1=h_rows[c][:],
-                op0=ALU.mult,
-                op1=ALU.add,
-            )
+            for part in parts_of(c):
+                nc.vector.scalar_tensor_tensor(
+                    out=y_rows[c][:, part, :],
+                    in0=k_rows[c][:, part, :],
+                    scalar=spread_times[:, 0:1],
+                    in1=h_rows[c][:, part, :],
+                    op0=ALU.mult,
+                    op1=ALU.add,
+                )
 
         def turn_y(c):
             y_grouped[c] = work.tile(
@@ -207,9 +218,17 @@ def tile_nodelstmcell_pb_t_kernel(tc, h_tilde, k_prev, t0, t1, W1, b1, W2, b2, o
                 waiting.append((c, s, summed))
 
         ctx.enter_context(tc.manual_schedule())
+        spread = scalar_banks.tile([P, 2 * TIME_GAP], F32, tag="bank")
+        nc.tensor.matmul(spread[:], lhsT=halves_signed[:], rhs=times[:], start=True, stop=True)
+        spread_times = const.tile([P, 2 * TIME_GAP], F32)
+        nc.vector.tensor_copy(out=spread_times[:], in_=spread[:])
         combine(0)
         w1_grouped = const.tile([P, WIDTH, PACK], BF16, align_bytes=64)
         turn(w1_rows, PACK, w1_grouped, halves)
+        spread_b2 = scalar_banks.tile([P, WIDTH], F32, tag="bank")
+        nc.tensor.matmul(spread_b2[:], lhsT=ones[:], rhs=b2_row[:], start=True, stop=True)
+        b2_all = const.tile([P, WIDTH], F32)
+        nc.scalar.copy(out=b2_all[:], in_=spread_b2[:])
         turn_y(0)
         combine(1)
         turn_y(1)
@@ -218,7 +237,7 @@ def tile_nodelstmcell_pb_t_kernel(tc, h_tilde, k_prev, t0, t1, W1, b1, W2, b2, o
         nc.vector.scalar_tensor_tensor(
             out=bias1[:],
             in0=w1_rows[:, :, WIDTH],
-            scalar=t_mid[:, 0:1],
+            scalar=spread_times[:, TIME_GAP : TIME_GAP + 1],
             in1=b1_cols[:],
             op0=ALU.mult,
             op1=ALU.add,

@@ -20,8 +20,7 @@ N_CHUNKS = len(CHUNK_ROWS)
 SLOTS_IN_BANK = 2
 PAIRS = PACK // 2
 
-Z_PART_ON_VECTOR = (1 / 4,) * 4 + (3 / 8,) * 4 + (1,)
-TIME_GAP = 16
+Z_PART_ON_VECTOR = (0,) + (3 / 8,) * 6 + (0, 0)
 VECTOR_BANKS = 4
 Y_LEAD = 4
 CHUNKS_IN_HALVES = 2
@@ -52,38 +51,43 @@ def tile_nodelstmcell_pb_t_kernel(tc, h_tilde, k_prev, t0, t1, W1, b1, W2, b2, o
         scalar_banks = ctx.enter_context(tc.psum_pool(name="scalar_banks", bufs=4))
         vector_banks = ctx.enter_context(tc.psum_pool(name="vector_banks", bufs=VECTOR_BANKS))
 
-        times = const.tile([P, 2 * TIME_GAP], BF16)
-        halves_signed = const.tile([P, P], BF16)
+        ctx.enter_context(tc.manual_schedule())
+
+        times = const.tile([P, 1], BF16)
+        plus_halves = const.tile([P, P], BF16)
+        signed_halves = const.tile([P, P], BF16)
         ones = const.tile([P, P], BF16)
         b2_row = const.tile([P, WIDTH], BF16)
         nc.vector.memset(times[:], 0.0)
-        nc.vector.memset(halves_signed[:], 0.5)
-        nc.vector.memset(halves_signed[32:64, :], -0.5)
+        nc.vector.memset(signed_halves[:], 0.5)
+        nc.vector.memset(signed_halves[32:64, :], -0.5)
+        nc.vector.memset(plus_halves[:], 0.5)
         nc.vector.memset(b2_row[:], 0.0)
         nc.vector.memset(ones[:], 1.0)
-        for time, row, col in ((t1, 0, 0), (t0, 32, 0), (t1, 0, TIME_GAP), (t0, 64, TIME_GAP)):
-            nc.scalar.dma_start(
-                out=times[row : row + 1, col : col + 1], in_=time.rearrange("(o n) -> o n", o=1)
-            )
-        b1_cols = const.tile([P, PACK], BF16)
-        nc.scalar.dma_start(out=b1_cols[:], in_=b1.rearrange("(m t) -> m t", t=PACK))
-        nc.scalar.dma_start(out=b2_row[0:1, :], in_=b2.rearrange("(o n) -> o n", o=1))
 
+        nc.sync.dma_start(out=times[0:1, :], in_=t1.rearrange("(o n) -> o n", o=1))
+        nc.sync.dma_start(out=times[32:33, :], in_=t0.rearrange("(o n) -> o n", o=1))
         w1_rows = const.tile([P, PACK, WIDTH + 2], BF16)
         w2_rows = const.tile([P, PACK, WIDTH], BF16)
+        b1_cols = const.tile([P, PACK], BF16)
         h_rows = []
         k_rows = []
-        nc.sync.dma_start(
-            out=w1_rows[:, :, 0 : WIDTH + 1], in_=W1.rearrange("(m r) k -> m r k", r=PACK)
-        )
         for c in range(N_CHUNKS):
             h_rows.append(inputs.tile([P, slots_of(c), WIDTH], BF16, name="h_rows"))
             k_rows.append(inputs.tile([P, slots_of(c), WIDTH], BF16, name="k_rows"))
-            for part in parts_of(c):
+            for i, part in enumerate(parts_of(c)):
                 nc.sync.dma_start(out=h_rows[c][:, part, :], in_=chunk_view(h_tilde, c)[:, part, :])
                 nc.sync.dma_start(out=k_rows[c][:, part, :], in_=chunk_view(k_prev, c)[:, part, :])
+                if c == 0 and i == 0:
+                    nc.sync.dma_start(
+                        out=w1_rows[:, :, 0 : WIDTH + 1],
+                        in_=W1.rearrange("(m r) k -> m r k", r=PACK),
+                    )
+            if c == 0:
+                nc.sync.dma_start(out=b1_cols[:], in_=b1.rearrange("(m t) -> m t", t=PACK))
             if c == 2:
                 nc.sync.dma_start(out=w2_rows[:], in_=W2.rearrange("(r m) k -> m r k", m=P))
+                nc.sync.dma_start(out=b2_row[0:1, :], in_=b2.rearrange("(o n) -> o n", o=1))
 
         identity = const.tile([P, P], F32)
         make_identity(nc, identity[:])
@@ -217,18 +221,16 @@ def tile_nodelstmcell_pb_t_kernel(tc, h_tilde, k_prev, t0, t1, W1, b1, W2, b2, o
                 multiply(summed[:], z_mx, slice(s * P, (s + 1) * P), w2_mx)
                 waiting.append((c, s, summed))
 
-        ctx.enter_context(tc.manual_schedule())
-        spread = scalar_banks.tile([P, 2 * TIME_GAP], F32, tag="bank")
-        nc.tensor.matmul(spread[:], lhsT=halves_signed[:], rhs=times[:], start=True, stop=True)
-        spread_times = const.tile([P, 2 * TIME_GAP], F32)
+        spread = scalar_banks.tile([P, 2], F32, tag="bank")
+        for i, halves_tile in enumerate((signed_halves, plus_halves)):
+            nc.tensor.matmul(
+                spread[:, i : i + 1], lhsT=halves_tile[:], rhs=times[:], start=True, stop=True
+            )
+        spread_times = const.tile([P, 2], F32)
         nc.vector.tensor_copy(out=spread_times[:], in_=spread[:])
         combine(0)
         w1_grouped = const.tile([P, WIDTH, PACK], BF16, align_bytes=64)
         turn(w1_rows, PACK, w1_grouped, halves)
-        spread_b2 = scalar_banks.tile([P, WIDTH], F32, tag="bank")
-        nc.tensor.matmul(spread_b2[:], lhsT=ones[:], rhs=b2_row[:], start=True, stop=True)
-        b2_all = const.tile([P, WIDTH], F32)
-        nc.scalar.copy(out=b2_all[:], in_=spread_b2[:])
         turn_y(0)
         combine(1)
         turn_y(1)
@@ -237,13 +239,14 @@ def tile_nodelstmcell_pb_t_kernel(tc, h_tilde, k_prev, t0, t1, W1, b1, W2, b2, o
         nc.vector.scalar_tensor_tensor(
             out=bias1[:],
             in0=w1_rows[:, :, WIDTH],
-            scalar=spread_times[:, TIME_GAP : TIME_GAP + 1],
+            scalar=spread_times[:, 1:2],
             in1=b1_cols[:],
             op0=ALU.mult,
             op1=ALU.add,
         )
 
         w2_grouped = const.tile([P, WIDTH, PACK], BF16, align_bytes=64)
+        b2_all = const.tile([P, WIDTH], F32)
         quantise_y(0)
         hidden_sums(0)
         for c in range(2, Y_LEAD):
@@ -255,6 +258,11 @@ def tile_nodelstmcell_pb_t_kernel(tc, h_tilde, k_prev, t0, t1, W1, b1, W2, b2, o
                 turn_y(c + 2)
             if c == 0:
                 turn(w2_rows, PACK, w2_grouped, alternate)
+                spread_b2 = scalar_banks.tile([P, WIDTH], F32, tag="bank")
+                nc.tensor.matmul(
+                    spread_b2[:], lhsT=ones[:], rhs=b2_row[:], start=True, stop=True
+                )
+                nc.scalar.copy(out=b2_all[:], in_=spread_b2[:])
             if c + 1 < N_CHUNKS:
                 quantise_y(c + 1)
             if c == 0:

@@ -20,7 +20,7 @@ N_CHUNKS = len(CHUNK_ROWS)
 SLOTS_IN_BANK = 2
 PAIRS = PACK // 2
 
-Z_PART_ON_VECTOR = (0,) + (3 / 8,) * 6 + (0, 0)
+Z_PART_ON_VECTOR = (0,) + (5 / 16,) * 6 + (0, 0)
 VECTOR_BANKS = 4
 Y_LEAD = 4
 CHUNKS_IN_HALVES = 2
@@ -59,10 +59,10 @@ def tile_nodelstmcell_pb_t_kernel(tc, h_tilde, k_prev, t0, t1, W1, b1, W2, b2, o
         ones = const.tile([P, P], BF16)
         b2_row = const.tile([P, WIDTH], BF16)
         nc.vector.memset(times[:], 0.0)
+        nc.vector.memset(b2_row[:], 0.0)
         nc.vector.memset(signed_halves[:], 0.5)
         nc.vector.memset(signed_halves[32:64, :], -0.5)
         nc.vector.memset(plus_halves[:], 0.5)
-        nc.vector.memset(b2_row[:], 0.0)
         nc.vector.memset(ones[:], 1.0)
 
         nc.sync.dma_start(out=times[0:1, :], in_=t1.rearrange("(o n) -> o n", o=1))
@@ -83,11 +83,11 @@ def tile_nodelstmcell_pb_t_kernel(tc, h_tilde, k_prev, t0, t1, W1, b1, W2, b2, o
                         out=w1_rows[:, :, 0 : WIDTH + 1],
                         in_=W1.rearrange("(m r) k -> m r k", r=PACK),
                     )
+                    nc.sync.dma_start(out=b2_row[0:1, :], in_=b2.rearrange("(o n) -> o n", o=1))
             if c == 0:
                 nc.sync.dma_start(out=b1_cols[:], in_=b1.rearrange("(m t) -> m t", t=PACK))
             if c == 2:
                 nc.sync.dma_start(out=w2_rows[:], in_=W2.rearrange("(r m) k -> m r k", m=P))
-                nc.sync.dma_start(out=b2_row[0:1, :], in_=b2.rearrange("(o n) -> o n", o=1))
 
         identity = const.tile([P, P], F32)
         make_identity(nc, identity[:])
@@ -152,9 +152,10 @@ def tile_nodelstmcell_pb_t_kernel(tc, h_tilde, k_prev, t0, t1, W1, b1, W2, b2, o
         result = {}
         waiting = []
 
-        def combine(c):
-            y_rows[c] = work.tile([P, slots_of(c), WIDTH], BF16, name="y_rows")
-            for part in parts_of(c):
+        def combine(c, parts=None):
+            if c not in y_rows:
+                y_rows[c] = work.tile([P, slots_of(c), WIDTH], BF16, name="y_rows")
+            for part in parts or parts_of(c):
                 nc.vector.scalar_tensor_tensor(
                     out=y_rows[c][:, part, :],
                     in0=k_rows[c][:, part, :],
@@ -204,8 +205,16 @@ def tile_nodelstmcell_pb_t_kernel(tc, h_tilde, k_prev, t0, t1, W1, b1, W2, b2, o
         def finish_oldest_sum():
             c, s, summed = waiting[0]
             waiting[:] = waiting[1:]
-            nc.vector.tensor_add(out=result[c][:, s, :], in0=summed[:], in1=b2_all[:])
-            nc.sync.dma_start(out=chunk_view(out, c)[:, s, :], in_=result[c][:, s, :])
+            last = (c, s) == (N_CHUNKS - 1, slots_of(c) - 1)
+            pieces = 2 if last else 1
+            for i in range(pieces):
+                cols = slice(i * WIDTH // pieces, (i + 1) * WIDTH // pieces)
+                nc.vector.tensor_add(
+                    out=result[c][:, s, cols], in0=summed[:, cols], in1=b2_all[:, cols]
+                )
+                nc.sync.dma_start(
+                    out=chunk_view(out, c)[:, s, cols], in_=result[c][:, s, cols]
+                )
 
         def second_layer(c):
             if vector_cols(c) > 0:
@@ -228,7 +237,12 @@ def tile_nodelstmcell_pb_t_kernel(tc, h_tilde, k_prev, t0, t1, W1, b1, W2, b2, o
             )
         spread_times = const.tile([P, 2], F32)
         nc.vector.tensor_copy(out=spread_times[:], in_=spread[:])
-        combine(0)
+        combine(0, parts_of(0)[:1])
+        spread_b2 = scalar_banks.tile([P, WIDTH], F32, tag="bank")
+        nc.tensor.matmul(spread_b2[:], lhsT=ones[:], rhs=b2_row[:], start=True, stop=True)
+        b2_all = const.tile([P, WIDTH], F32)
+        nc.vector.tensor_copy(out=b2_all[:], in_=spread_b2[:])
+        combine(0, parts_of(0)[1:])
         w1_grouped = const.tile([P, WIDTH, PACK], BF16, align_bytes=64)
         turn(w1_rows, PACK, w1_grouped, halves)
         turn_y(0)
@@ -246,7 +260,6 @@ def tile_nodelstmcell_pb_t_kernel(tc, h_tilde, k_prev, t0, t1, W1, b1, W2, b2, o
         )
 
         w2_grouped = const.tile([P, WIDTH, PACK], BF16, align_bytes=64)
-        b2_all = const.tile([P, WIDTH], F32)
         quantise_y(0)
         hidden_sums(0)
         for c in range(2, Y_LEAD):
@@ -258,11 +271,6 @@ def tile_nodelstmcell_pb_t_kernel(tc, h_tilde, k_prev, t0, t1, W1, b1, W2, b2, o
                 turn_y(c + 2)
             if c == 0:
                 turn(w2_rows, PACK, w2_grouped, alternate)
-                spread_b2 = scalar_banks.tile([P, WIDTH], F32, tag="bank")
-                nc.tensor.matmul(
-                    spread_b2[:], lhsT=ones[:], rhs=b2_row[:], start=True, stop=True
-                )
-                nc.scalar.copy(out=b2_all[:], in_=spread_b2[:])
             if c + 1 < N_CHUNKS:
                 quantise_y(c + 1)
             if c == 0:

@@ -60,10 +60,12 @@ def tile_nodelstmcell_pb_t_kernel(tc, h_tilde, k_prev, t0, t1, W1, b1, W2, b2, o
         b2_row = const.tile([P, WIDTH], BF16)
         nc.vector.memset(times[:], 0.0)
         nc.vector.memset(b2_row[:], 0.0)
+        nc.vector.memset(ones[:], 1.0)
         nc.vector.memset(signed_halves[:], 0.5)
         nc.vector.memset(signed_halves[32:64, :], -0.5)
         nc.vector.memset(plus_halves[:], 0.5)
-        nc.vector.memset(ones[:], 1.0)
+        unread_factor = const.tile([P, WIDTH], BF16)
+        nc.gpsimd.memset(unread_factor[:], 1.0)
 
         nc.sync.dma_start(out=times[0:1, :], in_=t1.rearrange("(o n) -> o n", o=1))
         nc.sync.dma_start(out=times[32:33, :], in_=t0.rearrange("(o n) -> o n", o=1))
@@ -230,6 +232,14 @@ def tile_nodelstmcell_pb_t_kernel(tc, h_tilde, k_prev, t0, t1, W1, b1, W2, b2, o
                 multiply(summed[:], z_mx, slice(s * P, (s + 1) * P), w2_mx)
                 waiting.append((c, s, summed))
 
+        def keep_clock_up(n):
+            unread = vector_banks.tile([P, WIDTH], F32, name="summed")
+            for _ in range(n):
+                nc.tensor.matmul(
+                    unread[:], lhsT=ones[:], rhs=unread_factor[:], start=True, stop=True
+                )
+
+        keep_clock_up(2)
         spread = scalar_banks.tile([P, 2], F32, tag="bank")
         for i, halves_tile in enumerate((signed_halves, plus_halves)):
             nc.tensor.matmul(
@@ -237,6 +247,7 @@ def tile_nodelstmcell_pb_t_kernel(tc, h_tilde, k_prev, t0, t1, W1, b1, W2, b2, o
             )
         spread_times = const.tile([P, 2], F32)
         nc.vector.tensor_copy(out=spread_times[:], in_=spread[:])
+        keep_clock_up(3)
         combine(0, parts_of(0)[:1])
         spread_b2 = scalar_banks.tile([P, WIDTH], F32, tag="bank")
         nc.tensor.matmul(spread_b2[:], lhsT=ones[:], rhs=b2_row[:], start=True, stop=True)
@@ -245,9 +256,12 @@ def tile_nodelstmcell_pb_t_kernel(tc, h_tilde, k_prev, t0, t1, W1, b1, W2, b2, o
         combine(0, parts_of(0)[1:])
         w1_grouped = const.tile([P, WIDTH, PACK], BF16, align_bytes=64)
         turn(w1_rows, PACK, w1_grouped, halves)
+        keep_clock_up(1)
         turn_y(0)
+        keep_clock_up(1)
         combine(1)
         turn_y(1)
+        keep_clock_up(1)
         w1_mx = quantise(w1_grouped, WIDTH, const, "w1")
         bias1 = const.tile([P, PACK], F32)
         nc.vector.scalar_tensor_tensor(

@@ -20,7 +20,8 @@ N_CHUNKS = len(CHUNK_ROWS)
 SLOTS_IN_BANK = 2
 PAIRS = PACK // 2
 
-Z_PART_ON_VECTOR = (0,) + (5 / 16,) * 6 + (0, 0)
+Z_PART_ON_VECTOR = (0, 5 / 16) + (0,) * 7
+Z_PART_ON_GPSIMD = (0, 0) + (5 / 8,) * 5 + (1 / 2, 1 / 2)
 VECTOR_BANKS = 4
 Y_LEAD = 4
 CHUNKS_IN_HALVES = 2
@@ -179,6 +180,9 @@ def tile_nodelstmcell_pb_t_kernel(tc, h_tilde, k_prev, t0, t1, W1, b1, W2, b2, o
         def vector_cols(c):
             return int(CHUNK_ROWS[c] * Z_PART_ON_VECTOR[c])
 
+        def gpsimd_cols(c):
+            return int(CHUNK_ROWS[c] * Z_PART_ON_GPSIMD[c])
+
         def lay_out_z(copy, c, first, last):
             copy(
                 out=z_grouped[c][:, first:last, :].rearrange("p (c i) t -> p c t i", i=4),
@@ -218,10 +222,24 @@ def tile_nodelstmcell_pb_t_kernel(tc, h_tilde, k_prev, t0, t1, W1, b1, W2, b2, o
                     out=chunk_view(out, c)[:, s, cols], in_=result[c][:, s, cols]
                 )
 
+        def lay_out_z_beside_sums(c):
+            one = work.tile([P, 1], F32, name="one")
+            nc.vector.memset(one[:], 1.0)
+            first = vector_cols(c)
+            last = first + gpsimd_cols(c)
+            nc.gpsimd.tensor_scalar(
+                out=z_grouped[c][:, first:last, :].rearrange("p (c i) t -> p c t i", i=4),
+                in0=z_planes[c][:, :, first:last].rearrange("p t (c i) -> p c t i", i=4),
+                scalar1=one[:, 0:1],
+                scalar2=0.0,
+                op0=ALU.mult,
+                op1=ALU.add,
+            )
+
         def second_layer(c):
             if vector_cols(c) > 0:
                 lay_out_z(nc.vector.tensor_copy, c, 0, vector_cols(c))
-            for _ in range(min(2, len(waiting))):
+            while waiting:
                 finish_oldest_sum()
             z_mx = quantise(z_grouped[c], CHUNK_ROWS[c], work, "z")
             result[c] = work.tile([P, slots_of(c), WIDTH], F32, name="result")
@@ -291,11 +309,13 @@ def tile_nodelstmcell_pb_t_kernel(tc, h_tilde, k_prev, t0, t1, W1, b1, W2, b2, o
                 w2_mx = quantise(w2_grouped, WIDTH, const, "w2")
             if c + 1 < N_CHUNKS:
                 hidden_sums(c + 1)
+            if c < N_CHUNKS and gpsimd_cols(c) > 0:
+                lay_out_z_beside_sums(c)
             if c >= 1:
                 second_layer(c - 1)
             if c + Y_LEAD < N_CHUNKS:
                 combine(c + Y_LEAD)
-            if c < N_CHUNKS and vector_cols(c) < CHUNK_ROWS[c]:
-                lay_out_z(nc.scalar.copy, c, vector_cols(c), CHUNK_ROWS[c])
+            if c < N_CHUNKS and vector_cols(c) + gpsimd_cols(c) < CHUNK_ROWS[c]:
+                lay_out_z(nc.scalar.copy, c, vector_cols(c) + gpsimd_cols(c), CHUNK_ROWS[c])
         while waiting:
             finish_oldest_sum()

@@ -20,8 +20,8 @@ N_CHUNKS = len(CHUNK_ROWS)
 SLOTS_IN_BANK = 2
 PAIRS = PACK // 2
 
-Z_PART_ON_VECTOR = (0, 5 / 16) + (0,) * 7
-Z_PART_ON_GPSIMD = (0, 0) + (5 / 8,) * 5 + (1 / 2, 1 / 2)
+Z_PART_ON_GPSIMD = 3 / 4
+PRODUCT_SLOTS = (0, 0, 1, 1, 1, 1, 2, 1, 1)
 VECTOR_BANKS = 4
 Y_LEAD = 4
 CHUNKS_IN_HALVES = 2
@@ -55,18 +55,21 @@ def tile_nodelstmcell_pb_t_kernel(tc, h_tilde, k_prev, t0, t1, W1, b1, W2, b2, o
         ctx.enter_context(tc.manual_schedule())
 
         times = const.tile([P, 1], BF16)
-        plus_halves = const.tile([P, P], BF16)
-        signed_halves = const.tile([P, P], BF16)
+        both_halves = const.tile([P, P], BF16)
+        later_half = const.tile([P, P], BF16)
+        earlier_half = const.tile([P, P], BF16)
         ones = const.tile([P, P], BF16)
         b2_row = const.tile([P, WIDTH], BF16)
         nc.vector.memset(times[:], 0.0)
         nc.vector.memset(b2_row[:], 0.0)
+        nc.vector.memset(later_half[:], 0.0)
+        nc.vector.memset(later_half[0:32, :], 0.5)
+        nc.vector.memset(earlier_half[:], 0.0)
+        nc.vector.memset(earlier_half[32:64, :], -0.5)
+        nc.vector.memset(both_halves[:], 0.5)
         nc.vector.memset(ones[:], 1.0)
-        nc.vector.memset(signed_halves[:], 0.5)
-        nc.vector.memset(signed_halves[32:64, :], -0.5)
-        nc.vector.memset(plus_halves[:], 0.5)
-        unread_factor = const.tile([P, WIDTH], BF16)
-        nc.gpsimd.memset(unread_factor[:], 1.0)
+        identity_bf16 = const.tile([P, P], BF16)
+        make_identity(nc, identity_bf16[:])
 
         nc.sync.dma_start(out=times[0:1, :], in_=t1.rearrange("(o n) -> o n", o=1))
         nc.sync.dma_start(out=times[32:33, :], in_=t0.rearrange("(o n) -> o n", o=1))
@@ -155,10 +158,13 @@ def tile_nodelstmcell_pb_t_kernel(tc, h_tilde, k_prev, t0, t1, W1, b1, W2, b2, o
         result = {}
         waiting = []
 
+        def vector_slots(c):
+            return slots_of(c) - PRODUCT_SLOTS[c]
+
         def combine(c, parts=None):
             if c not in y_rows:
-                y_rows[c] = work.tile([P, slots_of(c), WIDTH], BF16, name="y_rows")
-            for part in parts or parts_of(c):
+                y_rows[c] = work.tile([P, slots_of(c), WIDTH], BF16, name="y_rows", bufs=6)
+            for part in parts or [slice(0, vector_slots(c))]:
                 nc.vector.scalar_tensor_tensor(
                     out=y_rows[c][:, part, :],
                     in0=k_rows[c][:, part, :],
@@ -172,22 +178,53 @@ def tile_nodelstmcell_pb_t_kernel(tc, h_tilde, k_prev, t0, t1, W1, b1, W2, b2, o
             y_grouped[c] = work.tile(
                 [P, CHUNK_ROWS[c], PACK], BF16, align_bytes=64, name="y_grouped"
             )
-            turn(y_rows[c], slots_of(c), y_grouped[c], halves)
+            turn(y_rows[c], vector_slots(c), y_grouped[c], halves)
+            for s in range(vector_slots(c), slots_of(c)):
+                summed = scalar_banks.tile([P, PACK, P], F32, tag="bank")
+                for t in range(PACK):
+                    u, e = divmod(t, 2)
+                    cols = slice(2 * P * u + e, 2 * P * (u + 1), 2)
+                    terms = (
+                        (h_rows[c], identity_bf16),
+                        (k_rows[c], later_diagonal),
+                        (k_rows[c], earlier_diagonal),
+                    )
+                    for i, (rows, factor) in enumerate(terms):
+                        nc.tensor.matmul(
+                            summed[:, t, :],
+                            lhsT=rows[:, s, cols],
+                            rhs=factor[:],
+                            start=i == 0,
+                            stop=i == len(terms) - 1,
+                        )
+                nc.scalar.copy(
+                    out=y_grouped[c][:, s * P : (s + 1) * P, :],
+                    in_=summed[:].rearrange("p t n -> p n t"),
+                )
 
         def quantise_y(c):
             y_mx[c] = quantise(y_grouped[c], CHUNK_ROWS[c], work, "y")
 
-        def vector_cols(c):
-            return int(CHUNK_ROWS[c] * Z_PART_ON_VECTOR[c])
-
         def gpsimd_cols(c):
-            return int(CHUNK_ROWS[c] * Z_PART_ON_GPSIMD[c])
+            return int(CHUNK_ROWS[c] * Z_PART_ON_GPSIMD)
 
-        def lay_out_z(copy, c, first, last):
-            copy(
-                out=z_grouped[c][:, first:last, :].rearrange("p (c i) t -> p c t i", i=4),
-                in_=z_planes[c][:, :, first:last].rearrange("p t (c i) -> p c t i", i=4),
+        def z_views(c, first, last):
+            return (
+                z_grouped[c][:, first:last, :].rearrange("p (c i) t -> p c t i", i=4),
+                z_planes[c][:, :, first:last].rearrange("p t (c i) -> p c t i", i=4),
             )
+
+        def lay_out_z_on_gpsimd(c):
+            step = gpsimd_cols(c) // 2
+            for first in (0, step):
+                laid_out, planes = z_views(c, first, first + step)
+                nc.gpsimd.tensor_scalar(
+                    out=laid_out, in0=planes, scalar1=1.0, scalar2=0.0, op0=ALU.mult, op1=ALU.add
+                )
+
+        def lay_out_z_on_scalar(c):
+            laid_out, planes = z_views(c, gpsimd_cols(c), CHUNK_ROWS[c])
+            nc.scalar.copy(out=laid_out, in_=planes)
 
         def hidden_sums(c):
             hidden[c] = []
@@ -222,24 +259,8 @@ def tile_nodelstmcell_pb_t_kernel(tc, h_tilde, k_prev, t0, t1, W1, b1, W2, b2, o
                     out=chunk_view(out, c)[:, s, cols], in_=result[c][:, s, cols]
                 )
 
-        def lay_out_z_beside_sums(c):
-            one = work.tile([P, 1], F32, name="one")
-            nc.vector.memset(one[:], 1.0)
-            first = vector_cols(c)
-            last = first + gpsimd_cols(c)
-            nc.gpsimd.tensor_scalar(
-                out=z_grouped[c][:, first:last, :].rearrange("p (c i) t -> p c t i", i=4),
-                in0=z_planes[c][:, :, first:last].rearrange("p t (c i) -> p c t i", i=4),
-                scalar1=one[:, 0:1],
-                scalar2=0.0,
-                op0=ALU.mult,
-                op1=ALU.add,
-            )
-
         def second_layer(c):
-            if vector_cols(c) > 0:
-                lay_out_z(nc.vector.tensor_copy, c, 0, vector_cols(c))
-            while waiting:
+            for _ in range(min(2, len(waiting))):
                 finish_oldest_sum()
             z_mx = quantise(z_grouped[c], CHUNK_ROWS[c], work, "z")
             result[c] = work.tile([P, slots_of(c), WIDTH], F32, name="result")
@@ -250,36 +271,41 @@ def tile_nodelstmcell_pb_t_kernel(tc, h_tilde, k_prev, t0, t1, W1, b1, W2, b2, o
                 multiply(summed[:], z_mx, slice(s * P, (s + 1) * P), w2_mx)
                 waiting.append((c, s, summed))
 
-        def keep_clock_up(n):
-            unread = vector_banks.tile([P, WIDTH], F32, name="summed")
-            for _ in range(n):
+        spread = scalar_banks.tile([P, 4], F32, tag="bank")
+        for i, factors in enumerate(
+            ((later_half, earlier_half), (both_halves,), (later_half,), (earlier_half,))
+        ):
+            for j, factor in enumerate(factors):
                 nc.tensor.matmul(
-                    unread[:], lhsT=ones[:], rhs=unread_factor[:], start=True, stop=True
+                    spread[:, i : i + 1],
+                    lhsT=factor[:],
+                    rhs=times[:],
+                    start=j == 0,
+                    stop=j == len(factors) - 1,
                 )
-
-        keep_clock_up(2)
-        spread = scalar_banks.tile([P, 2], F32, tag="bank")
-        for i, halves_tile in enumerate((signed_halves, plus_halves)):
-            nc.tensor.matmul(
-                spread[:, i : i + 1], lhsT=halves_tile[:], rhs=times[:], start=True, stop=True
-            )
-        spread_times = const.tile([P, 2], F32)
+        spread_times = const.tile([P, 4], F32)
         nc.vector.tensor_copy(out=spread_times[:], in_=spread[:])
-        keep_clock_up(3)
+        later_diagonal = const.tile([P, P], BF16)
+        earlier_diagonal = const.tile([P, P], BF16)
+        for i, diagonal in ((2, later_diagonal), (3, earlier_diagonal)):
+            nc.gpsimd.tensor_scalar(
+                out=diagonal[:],
+                in0=identity_bf16[:],
+                scalar1=spread_times[:, i : i + 1],
+                scalar2=0.0,
+                op0=ALU.mult,
+                op1=ALU.add,
+            )
         combine(0, parts_of(0)[:1])
         spread_b2 = scalar_banks.tile([P, WIDTH], F32, tag="bank")
         nc.tensor.matmul(spread_b2[:], lhsT=ones[:], rhs=b2_row[:], start=True, stop=True)
         b2_all = const.tile([P, WIDTH], F32)
-        nc.vector.tensor_copy(out=b2_all[:], in_=spread_b2[:])
+        nc.scalar.copy(out=b2_all[:], in_=spread_b2[:])
         combine(0, parts_of(0)[1:])
         w1_grouped = const.tile([P, WIDTH, PACK], BF16, align_bytes=64)
         turn(w1_rows, PACK, w1_grouped, halves)
-        keep_clock_up(1)
         turn_y(0)
-        keep_clock_up(1)
-        combine(1)
-        turn_y(1)
-        keep_clock_up(1)
+        combine(1, parts_of(1)[:1])
         w1_mx = quantise(w1_grouped, WIDTH, const, "w1")
         bias1 = const.tile([P, PACK], F32)
         nc.vector.scalar_tensor_tensor(
@@ -290,32 +316,36 @@ def tile_nodelstmcell_pb_t_kernel(tc, h_tilde, k_prev, t0, t1, W1, b1, W2, b2, o
             op0=ALU.mult,
             op1=ALU.add,
         )
-
-        w2_grouped = const.tile([P, WIDTH, PACK], BF16, align_bytes=64)
         quantise_y(0)
         hidden_sums(0)
-        for c in range(2, Y_LEAD):
-            combine(c)
-        for c in range(N_CHUNKS + 1):
+        combine(1, parts_of(1)[1:])
+        hidden_tanh(0)
+        turn_y(1)
+        combine(2)
+        turn_y(2)
+        w2_grouped = const.tile([P, WIDTH, PACK], BF16, align_bytes=64)
+        turn(w2_rows, PACK, w2_grouped, alternate)
+        quantise_y(1)
+        hidden_sums(1)
+        combine(3)
+        w2_mx = quantise(w2_grouped, WIDTH, const, "w2")
+        lay_out_z_on_gpsimd(0)
+        combine(4)
+        lay_out_z_on_scalar(0)
+        for c in range(1, N_CHUNKS + 1):
             if c < N_CHUNKS:
                 hidden_tanh(c)
             if c + 2 < N_CHUNKS:
                 turn_y(c + 2)
-            if c == 0:
-                turn(w2_rows, PACK, w2_grouped, alternate)
             if c + 1 < N_CHUNKS:
                 quantise_y(c + 1)
-            if c == 0:
-                w2_mx = quantise(w2_grouped, WIDTH, const, "w2")
-            if c + 1 < N_CHUNKS:
                 hidden_sums(c + 1)
-            if c < N_CHUNKS and gpsimd_cols(c) > 0:
-                lay_out_z_beside_sums(c)
-            if c >= 1:
-                second_layer(c - 1)
+            if c < N_CHUNKS:
+                lay_out_z_on_gpsimd(c)
+            second_layer(c - 1)
             if c + Y_LEAD < N_CHUNKS:
                 combine(c + Y_LEAD)
-            if c < N_CHUNKS and vector_cols(c) + gpsimd_cols(c) < CHUNK_ROWS[c]:
-                lay_out_z(nc.scalar.copy, c, vector_cols(c) + gpsimd_cols(c), CHUNK_ROWS[c])
+            if c < N_CHUNKS:
+                lay_out_z_on_scalar(c)
         while waiting:
             finish_oldest_sum()

@@ -20,8 +20,7 @@ N_CHUNKS = len(CHUNK_ROWS)
 SLOTS_IN_BANK = 2
 PAIRS = PACK // 2
 
-Z_PART_ON_GPSIMD = 3 / 4
-PRODUCT_SLOTS = (0, 0, 1, 1, 1, 1, 2, 1, 1)
+Z_PART_ON_GPSIMD = 3 / 8
 VECTOR_BANKS = 4
 Y_LEAD = 4
 CHUNKS_IN_HALVES = 2
@@ -55,21 +54,16 @@ def tile_nodelstmcell_pb_t_kernel(tc, h_tilde, k_prev, t0, t1, W1, b1, W2, b2, o
         ctx.enter_context(tc.manual_schedule())
 
         times = const.tile([P, 1], BF16)
-        both_halves = const.tile([P, P], BF16)
-        later_half = const.tile([P, P], BF16)
-        earlier_half = const.tile([P, P], BF16)
+        plus_halves = const.tile([P, P], BF16)
+        signed_halves = const.tile([P, P], BF16)
         ones = const.tile([P, P], BF16)
         b2_row = const.tile([P, WIDTH], BF16)
         nc.vector.memset(times[:], 0.0)
         nc.vector.memset(b2_row[:], 0.0)
-        nc.vector.memset(later_half[:], 0.0)
-        nc.vector.memset(later_half[0:32, :], 0.5)
-        nc.vector.memset(earlier_half[:], 0.0)
-        nc.vector.memset(earlier_half[32:64, :], -0.5)
-        nc.vector.memset(both_halves[:], 0.5)
         nc.vector.memset(ones[:], 1.0)
-        identity_bf16 = const.tile([P, P], BF16)
-        make_identity(nc, identity_bf16[:])
+        nc.vector.memset(signed_halves[:], 0.5)
+        nc.vector.memset(signed_halves[32:64, :], -0.5)
+        nc.vector.memset(plus_halves[:], 0.5)
 
         nc.sync.dma_start(out=times[0:1, :], in_=t1.rearrange("(o n) -> o n", o=1))
         nc.sync.dma_start(out=times[32:33, :], in_=t0.rearrange("(o n) -> o n", o=1))
@@ -158,13 +152,10 @@ def tile_nodelstmcell_pb_t_kernel(tc, h_tilde, k_prev, t0, t1, W1, b1, W2, b2, o
         result = {}
         waiting = []
 
-        def vector_slots(c):
-            return slots_of(c) - PRODUCT_SLOTS[c]
-
         def combine(c, parts=None):
             if c not in y_rows:
                 y_rows[c] = work.tile([P, slots_of(c), WIDTH], BF16, name="y_rows", bufs=6)
-            for part in parts or [slice(0, vector_slots(c))]:
+            for part in parts or [slice(0, slots_of(c))]:
                 nc.vector.scalar_tensor_tensor(
                     out=y_rows[c][:, part, :],
                     in0=k_rows[c][:, part, :],
@@ -178,29 +169,7 @@ def tile_nodelstmcell_pb_t_kernel(tc, h_tilde, k_prev, t0, t1, W1, b1, W2, b2, o
             y_grouped[c] = work.tile(
                 [P, CHUNK_ROWS[c], PACK], BF16, align_bytes=64, name="y_grouped"
             )
-            turn(y_rows[c], vector_slots(c), y_grouped[c], halves)
-            for s in range(vector_slots(c), slots_of(c)):
-                summed = scalar_banks.tile([P, PACK, P], F32, tag="bank")
-                for t in range(PACK):
-                    u, e = divmod(t, 2)
-                    cols = slice(2 * P * u + e, 2 * P * (u + 1), 2)
-                    terms = (
-                        (h_rows[c], identity_bf16),
-                        (k_rows[c], later_diagonal),
-                        (k_rows[c], earlier_diagonal),
-                    )
-                    for i, (rows, factor) in enumerate(terms):
-                        nc.tensor.matmul(
-                            summed[:, t, :],
-                            lhsT=rows[:, s, cols],
-                            rhs=factor[:],
-                            start=i == 0,
-                            stop=i == len(terms) - 1,
-                        )
-                nc.scalar.copy(
-                    out=y_grouped[c][:, s * P : (s + 1) * P, :],
-                    in_=summed[:].rearrange("p t n -> p n t"),
-                )
+            turn(y_rows[c], slots_of(c), y_grouped[c], halves)
 
         def quantise_y(c):
             y_mx[c] = quantise(y_grouped[c], CHUNK_ROWS[c], work, "y")
@@ -260,8 +229,6 @@ def tile_nodelstmcell_pb_t_kernel(tc, h_tilde, k_prev, t0, t1, W1, b1, W2, b2, o
                 )
 
         def second_layer(c):
-            for _ in range(min(2, len(waiting))):
-                finish_oldest_sum()
             z_mx = quantise(z_grouped[c], CHUNK_ROWS[c], work, "z")
             result[c] = work.tile([P, slots_of(c), WIDTH], F32, name="result")
             for s in range(slots_of(c)):
@@ -271,31 +238,13 @@ def tile_nodelstmcell_pb_t_kernel(tc, h_tilde, k_prev, t0, t1, W1, b1, W2, b2, o
                 multiply(summed[:], z_mx, slice(s * P, (s + 1) * P), w2_mx)
                 waiting.append((c, s, summed))
 
-        spread = scalar_banks.tile([P, 4], F32, tag="bank")
-        for i, factors in enumerate(
-            ((later_half, earlier_half), (both_halves,), (later_half,), (earlier_half,))
-        ):
-            for j, factor in enumerate(factors):
-                nc.tensor.matmul(
-                    spread[:, i : i + 1],
-                    lhsT=factor[:],
-                    rhs=times[:],
-                    start=j == 0,
-                    stop=j == len(factors) - 1,
-                )
-        spread_times = const.tile([P, 4], F32)
-        nc.vector.tensor_copy(out=spread_times[:], in_=spread[:])
-        later_diagonal = const.tile([P, P], BF16)
-        earlier_diagonal = const.tile([P, P], BF16)
-        for i, diagonal in ((2, later_diagonal), (3, earlier_diagonal)):
-            nc.gpsimd.tensor_scalar(
-                out=diagonal[:],
-                in0=identity_bf16[:],
-                scalar1=spread_times[:, i : i + 1],
-                scalar2=0.0,
-                op0=ALU.mult,
-                op1=ALU.add,
+        spread = scalar_banks.tile([P, 2], F32, tag="bank")
+        for i, halves_tile in enumerate((signed_halves, plus_halves)):
+            nc.tensor.matmul(
+                spread[:, i : i + 1], lhsT=halves_tile[:], rhs=times[:], start=True, stop=True
             )
+        spread_times = const.tile([P, 2], F32)
+        nc.vector.tensor_copy(out=spread_times[:], in_=spread[:])
         combine(0, parts_of(0)[:1])
         spread_b2 = scalar_banks.tile([P, WIDTH], F32, tag="bank")
         nc.tensor.matmul(spread_b2[:], lhsT=ones[:], rhs=b2_row[:], start=True, stop=True)

@@ -20,7 +20,8 @@ N_CHUNKS = len(CHUNK_ROWS)
 SLOTS_IN_BANK = 2
 PAIRS = PACK // 2
 
-Z_PART_ON_GPSIMD = 3 / 8
+Z_PART_ON_VECTOR = (0, 1 / 4) + (0,) * 7
+Z_PART_ON_GPSIMD = (0, 0) + (1 / 2,) * 5 + (1 / 4, 1 / 4)
 VECTOR_BANKS = 4
 Y_LEAD = 4
 CHUNKS_IN_HALVES = 2
@@ -175,7 +176,10 @@ def tile_nodelstmcell_pb_t_kernel(tc, h_tilde, k_prev, t0, t1, W1, b1, W2, b2, o
             y_mx[c] = quantise(y_grouped[c], CHUNK_ROWS[c], work, "y")
 
         def gpsimd_cols(c):
-            return int(CHUNK_ROWS[c] * Z_PART_ON_GPSIMD)
+            return int(CHUNK_ROWS[c] * Z_PART_ON_GPSIMD[c])
+
+        def vector_cols(c):
+            return int(CHUNK_ROWS[c] * Z_PART_ON_VECTOR[c])
 
         def z_views(c, first, last):
             return (
@@ -184,15 +188,24 @@ def tile_nodelstmcell_pb_t_kernel(tc, h_tilde, k_prev, t0, t1, W1, b1, W2, b2, o
             )
 
         def lay_out_z_on_gpsimd(c):
-            step = gpsimd_cols(c) // 2
-            for first in (0, step):
-                laid_out, planes = z_views(c, first, first + step)
-                nc.gpsimd.tensor_scalar(
-                    out=laid_out, in0=planes, scalar1=1.0, scalar2=0.0, op0=ALU.mult, op1=ALU.add
-                )
+            one = work.tile([P, 1], F32, name="one")
+            nc.vector.memset(one[:], 1.0)
+            laid_out, planes = z_views(c, 0, gpsimd_cols(c))
+            nc.gpsimd.tensor_scalar(
+                out=laid_out,
+                in0=planes,
+                scalar1=one[:, 0:1],
+                scalar2=0.0,
+                op0=ALU.mult,
+                op1=ALU.add,
+            )
+
+        def lay_out_z_on_vector(c):
+            laid_out, planes = z_views(c, gpsimd_cols(c), gpsimd_cols(c) + vector_cols(c))
+            nc.vector.tensor_copy(out=laid_out, in_=planes)
 
         def lay_out_z_on_scalar(c):
-            laid_out, planes = z_views(c, gpsimd_cols(c), CHUNK_ROWS[c])
+            laid_out, planes = z_views(c, gpsimd_cols(c) + vector_cols(c), CHUNK_ROWS[c])
             nc.scalar.copy(out=laid_out, in_=planes)
 
         def hidden_sums(c):
@@ -229,7 +242,11 @@ def tile_nodelstmcell_pb_t_kernel(tc, h_tilde, k_prev, t0, t1, W1, b1, W2, b2, o
                 )
 
         def second_layer(c):
+            if vector_cols(c) > 0:
+                lay_out_z_on_vector(c)
             z_mx = quantise(z_grouped[c], CHUNK_ROWS[c], work, "z")
+            if c + 1 < N_CHUNKS and gpsimd_cols(c + 1) > 0:
+                lay_out_z_on_gpsimd(c + 1)
             result[c] = work.tile([P, slots_of(c), WIDTH], F32, name="result")
             for s in range(slots_of(c)):
                 if len(waiting) == VECTOR_BANKS:
@@ -278,7 +295,6 @@ def tile_nodelstmcell_pb_t_kernel(tc, h_tilde, k_prev, t0, t1, W1, b1, W2, b2, o
         hidden_sums(1)
         combine(3)
         w2_mx = quantise(w2_grouped, WIDTH, const, "w2")
-        lay_out_z_on_gpsimd(0)
         combine(4)
         lay_out_z_on_scalar(0)
         for c in range(1, N_CHUNKS + 1):
@@ -289,8 +305,6 @@ def tile_nodelstmcell_pb_t_kernel(tc, h_tilde, k_prev, t0, t1, W1, b1, W2, b2, o
             if c + 1 < N_CHUNKS:
                 quantise_y(c + 1)
                 hidden_sums(c + 1)
-            if c < N_CHUNKS:
-                lay_out_z_on_gpsimd(c)
             second_layer(c - 1)
             if c + Y_LEAD < N_CHUNKS:
                 combine(c + Y_LEAD)

@@ -21,7 +21,8 @@ SLOTS_IN_BANK = 2
 PAIRS = PACK // 2
 
 Z_PART_ON_VECTOR = (0, 1 / 4) + (0,) * 7
-Z_PART_ON_GPSIMD = (0, 0) + (1 / 2,) * 5 + (1 / 4, 1 / 4)
+Z_PART_ON_GPSIMD = (0, 1 / 2) + (5 / 8,) * 5 + (1 / 4, 1 / 4)
+PRODUCT_SLOTS = (0,) * 4 + (1,) * 3 + (0,) * 2
 VECTOR_BANKS = 4
 Y_LEAD = 4
 CHUNKS_IN_HALVES = 2
@@ -55,16 +56,23 @@ def tile_nodelstmcell_pb_t_kernel(tc, h_tilde, k_prev, t0, t1, W1, b1, W2, b2, o
         ctx.enter_context(tc.manual_schedule())
 
         times = const.tile([P, 1], BF16)
-        plus_halves = const.tile([P, P], BF16)
-        signed_halves = const.tile([P, P], BF16)
+        both_halves = const.tile([P, P], BF16)
+        later_half = const.tile([P, P], BF16)
+        earlier_half = const.tile([P, P], BF16)
         ones = const.tile([P, P], BF16)
         b2_row = const.tile([P, WIDTH], BF16)
         nc.vector.memset(times[:], 0.0)
         nc.vector.memset(b2_row[:], 0.0)
         nc.vector.memset(ones[:], 1.0)
-        nc.vector.memset(signed_halves[:], 0.5)
-        nc.vector.memset(signed_halves[32:64, :], -0.5)
-        nc.vector.memset(plus_halves[:], 0.5)
+        nc.vector.memset(later_half[:], 0.0)
+        nc.vector.memset(later_half[0:32, :], 0.5)
+        nc.vector.memset(earlier_half[:], 0.0)
+        nc.vector.memset(earlier_half[32:64, :], -0.5)
+        nc.vector.memset(both_halves[:], 0.5)
+        unread_factor = const.tile([P, WIDTH], BF16)
+        nc.gpsimd.memset(unread_factor[:], 1.0)
+        identity_bf16 = const.tile([P, P], BF16)
+        make_identity(nc, identity_bf16[:])
 
         nc.sync.dma_start(out=times[0:1, :], in_=t1.rearrange("(o n) -> o n", o=1))
         nc.sync.dma_start(out=times[32:33, :], in_=t0.rearrange("(o n) -> o n", o=1))
@@ -153,10 +161,14 @@ def tile_nodelstmcell_pb_t_kernel(tc, h_tilde, k_prev, t0, t1, W1, b1, W2, b2, o
         result = {}
         waiting = []
 
+        def vector_slots(c):
+            return slots_of(c) - PRODUCT_SLOTS[c]
+
         def combine(c, parts=None):
             if c not in y_rows:
-                y_rows[c] = work.tile([P, slots_of(c), WIDTH], BF16, name="y_rows", bufs=6)
-            for part in parts or [slice(0, slots_of(c))]:
+                y_rows[c] = work.tile([P, slots_of(c), WIDTH], BF16, name="y_rows")
+            for part in parts or parts_of(c):
+                part = slice(part.start, min(part.stop, vector_slots(c)))
                 nc.vector.scalar_tensor_tensor(
                     out=y_rows[c][:, part, :],
                     in0=k_rows[c][:, part, :],
@@ -170,16 +182,38 @@ def tile_nodelstmcell_pb_t_kernel(tc, h_tilde, k_prev, t0, t1, W1, b1, W2, b2, o
             y_grouped[c] = work.tile(
                 [P, CHUNK_ROWS[c], PACK], BF16, align_bytes=64, name="y_grouped"
             )
-            turn(y_rows[c], slots_of(c), y_grouped[c], halves)
+            for s in range(vector_slots(c), slots_of(c)):
+                summed = scalar_banks.tile([P, PACK, P], F32, tag="bank")
+                for t in range(PACK):
+                    u, e = divmod(t, 2)
+                    cols = slice(2 * P * u + e, 2 * P * (u + 1), 2)
+                    terms = (
+                        (h_rows[c], identity_bf16),
+                        (k_rows[c], later_diagonal),
+                        (k_rows[c], earlier_diagonal),
+                    )
+                    for i, (rows, factor) in enumerate(terms):
+                        nc.tensor.matmul(
+                            summed[:, t, :],
+                            lhsT=rows[:, s, cols],
+                            rhs=factor[:],
+                            start=i == 0,
+                            stop=i == len(terms) - 1,
+                        )
+                nc.scalar.copy(
+                    out=y_grouped[c][:, s * P : (s + 1) * P, :],
+                    in_=summed[:].rearrange("p t n -> p n t"),
+                )
+            turn(y_rows[c], vector_slots(c), y_grouped[c], halves)
 
         def quantise_y(c):
             y_mx[c] = quantise(y_grouped[c], CHUNK_ROWS[c], work, "y")
 
-        def gpsimd_cols(c):
-            return int(CHUNK_ROWS[c] * Z_PART_ON_GPSIMD[c])
-
         def vector_cols(c):
             return int(CHUNK_ROWS[c] * Z_PART_ON_VECTOR[c])
+
+        def gpsimd_cols(c):
+            return int(CHUNK_ROWS[c] * Z_PART_ON_GPSIMD[c])
 
         def z_views(c, first, last):
             return (
@@ -187,26 +221,22 @@ def tile_nodelstmcell_pb_t_kernel(tc, h_tilde, k_prev, t0, t1, W1, b1, W2, b2, o
                 z_planes[c][:, :, first:last].rearrange("p t (c i) -> p c t i", i=4),
             )
 
+        def lay_out_z(copy, c, first, last):
+            laid_out, planes = z_views(c, first, last)
+            copy(out=laid_out, in_=planes)
+
         def lay_out_z_on_gpsimd(c):
             one = work.tile([P, 1], F32, name="one")
             nc.vector.memset(one[:], 1.0)
-            laid_out, planes = z_views(c, 0, gpsimd_cols(c))
+            cols = slice(0, gpsimd_cols(c))
             nc.gpsimd.tensor_scalar(
-                out=laid_out,
-                in0=planes,
+                out=z_grouped[c][:, cols, :],
+                in0=z_planes[c][:, :, cols].rearrange("p t c -> p c t"),
                 scalar1=one[:, 0:1],
                 scalar2=0.0,
                 op0=ALU.mult,
                 op1=ALU.add,
             )
-
-        def lay_out_z_on_vector(c):
-            laid_out, planes = z_views(c, gpsimd_cols(c), gpsimd_cols(c) + vector_cols(c))
-            nc.vector.tensor_copy(out=laid_out, in_=planes)
-
-        def lay_out_z_on_scalar(c):
-            laid_out, planes = z_views(c, gpsimd_cols(c) + vector_cols(c), CHUNK_ROWS[c])
-            nc.scalar.copy(out=laid_out, in_=planes)
 
         def hidden_sums(c):
             hidden[c] = []
@@ -243,7 +273,7 @@ def tile_nodelstmcell_pb_t_kernel(tc, h_tilde, k_prev, t0, t1, W1, b1, W2, b2, o
 
         def second_layer(c):
             if vector_cols(c) > 0:
-                lay_out_z_on_vector(c)
+                lay_out_z(nc.vector.tensor_copy, c, gpsimd_cols(c), gpsimd_cols(c) + vector_cols(c))
             z_mx = quantise(z_grouped[c], CHUNK_ROWS[c], work, "z")
             if c + 1 < N_CHUNKS and gpsimd_cols(c + 1) > 0:
                 lay_out_z_on_gpsimd(c + 1)
@@ -255,23 +285,53 @@ def tile_nodelstmcell_pb_t_kernel(tc, h_tilde, k_prev, t0, t1, W1, b1, W2, b2, o
                 multiply(summed[:], z_mx, slice(s * P, (s + 1) * P), w2_mx)
                 waiting.append((c, s, summed))
 
-        spread = scalar_banks.tile([P, 2], F32, tag="bank")
-        for i, halves_tile in enumerate((signed_halves, plus_halves)):
-            nc.tensor.matmul(
-                spread[:, i : i + 1], lhsT=halves_tile[:], rhs=times[:], start=True, stop=True
-            )
-        spread_times = const.tile([P, 2], F32)
+        def keep_clock_up(n):
+            unread = vector_banks.tile([P, WIDTH], F32, name="summed")
+            for _ in range(n):
+                nc.tensor.matmul(
+                    unread[:], lhsT=ones[:], rhs=unread_factor[:], start=True, stop=True
+                )
+
+        spread = scalar_banks.tile([P, 4], F32, tag="bank")
+        for i, factors in enumerate(
+            ((later_half, earlier_half), (both_halves,), (later_half,), (earlier_half,))
+        ):
+            for j, factor in enumerate(factors):
+                nc.tensor.matmul(
+                    spread[:, i : i + 1],
+                    lhsT=factor[:],
+                    rhs=times[:],
+                    start=j == 0,
+                    stop=j == len(factors) - 1,
+                )
+        spread_times = const.tile([P, 4], F32)
         nc.vector.tensor_copy(out=spread_times[:], in_=spread[:])
+        later_diagonal = const.tile([P, P], BF16)
+        earlier_diagonal = const.tile([P, P], BF16)
+        for i, diagonal in ((2, later_diagonal), (3, earlier_diagonal)):
+            nc.gpsimd.tensor_scalar(
+                out=diagonal[:],
+                in0=identity_bf16[:],
+                scalar1=spread_times[:, i : i + 1],
+                scalar2=0.0,
+                op0=ALU.mult,
+                op1=ALU.add,
+            )
+        keep_clock_up(3)
         combine(0, parts_of(0)[:1])
         spread_b2 = scalar_banks.tile([P, WIDTH], F32, tag="bank")
         nc.tensor.matmul(spread_b2[:], lhsT=ones[:], rhs=b2_row[:], start=True, stop=True)
         b2_all = const.tile([P, WIDTH], F32)
-        nc.scalar.copy(out=b2_all[:], in_=spread_b2[:])
+        nc.vector.tensor_copy(out=b2_all[:], in_=spread_b2[:])
         combine(0, parts_of(0)[1:])
         w1_grouped = const.tile([P, WIDTH, PACK], BF16, align_bytes=64)
         turn(w1_rows, PACK, w1_grouped, halves)
+        keep_clock_up(1)
         turn_y(0)
-        combine(1, parts_of(1)[:1])
+        keep_clock_up(1)
+        combine(1)
+        turn_y(1)
+        keep_clock_up(1)
         w1_mx = quantise(w1_grouped, WIDTH, const, "w1")
         bias1 = const.tile([P, PACK], F32)
         nc.vector.scalar_tensor_tensor(
@@ -282,33 +342,30 @@ def tile_nodelstmcell_pb_t_kernel(tc, h_tilde, k_prev, t0, t1, W1, b1, W2, b2, o
             op0=ALU.mult,
             op1=ALU.add,
         )
+
+        w2_grouped = const.tile([P, WIDTH, PACK], BF16, align_bytes=64)
         quantise_y(0)
         hidden_sums(0)
-        combine(1, parts_of(1)[1:])
-        hidden_tanh(0)
-        turn_y(1)
-        combine(2)
-        turn_y(2)
-        w2_grouped = const.tile([P, WIDTH, PACK], BF16, align_bytes=64)
-        turn(w2_rows, PACK, w2_grouped, alternate)
-        quantise_y(1)
-        hidden_sums(1)
-        combine(3)
-        w2_mx = quantise(w2_grouped, WIDTH, const, "w2")
-        combine(4)
-        lay_out_z_on_scalar(0)
-        for c in range(1, N_CHUNKS + 1):
+        for c in range(2, Y_LEAD):
+            combine(c)
+        for c in range(N_CHUNKS + 1):
             if c < N_CHUNKS:
                 hidden_tanh(c)
             if c + 2 < N_CHUNKS:
                 turn_y(c + 2)
+            if c == 0:
+                turn(w2_rows, PACK, w2_grouped, alternate)
             if c + 1 < N_CHUNKS:
                 quantise_y(c + 1)
+            if c == 0:
+                w2_mx = quantise(w2_grouped, WIDTH, const, "w2")
+            if c + 1 < N_CHUNKS:
                 hidden_sums(c + 1)
-            second_layer(c - 1)
+            if c >= 1:
+                second_layer(c - 1)
             if c + Y_LEAD < N_CHUNKS:
                 combine(c + Y_LEAD)
             if c < N_CHUNKS:
-                lay_out_z_on_scalar(c)
+                lay_out_z(nc.scalar.copy, c, vector_cols(c) + gpsimd_cols(c), CHUNK_ROWS[c])
         while waiting:
             finish_oldest_sum()

from contextlib import ExitStack

import concourse.mybir as mybir
from concourse.masks import make_identity

BF16 = mybir.dt.bfloat16
F32 = mybir.dt.float32
U32 = mybir.dt.uint32
U8 = mybir.dt.uint8
FP8X4 = mybir.dt.float8_e4m3fn_x4
ALU = mybir.AluOpType
ACT = mybir.ActivationFunctionType

P = 128
PACK = 4
WIDTH = P * PACK
BATCH = 4096
CHUNK_ROWS = (512,) * 7 + (256, 256)
N_CHUNKS = len(CHUNK_ROWS)
SLOTS_IN_BANK = 2
PAIRS = PACK // 2

Z_PART_ON_VECTOR = (0, 1 / 4) + (0,) * 7
Z_PART_ON_GPSIMD = (0, 1 / 2) + (5 / 8,) * 5 + (1 / 4, 1 / 4)
PRODUCT_SLOTS = (0,) * 4 + (1,) * 3 + (0,) * 2
VECTOR_BANKS = 4
Y_LEAD = 4
CHUNKS_IN_HALVES = 2

FLOPS = 2 * 2 * BATCH * WIDTH * WIDTH


def tile_nodelstmcell_pb_t_kernel(tc, h_tilde, k_prev, t0, t1, W1, b1, W2, b2, out):
    nc = tc.nc

    def chunk_view(x, c):
        first = sum(CHUNK_ROWS[:c])
        rows = x[first : first + CHUNK_ROWS[c], :]
        return rows.rearrange("(q s) k -> q s k", q=P)

    def slots_of(c):
        return CHUNK_ROWS[c] // P

    def parts_of(c):
        slots = slots_of(c)
        step = slots // 2 if c < CHUNKS_IN_HALVES else slots
        return [slice(s, s + step) for s in range(0, slots, step)]

    with ExitStack() as ctx:
        const = ctx.enter_context(tc.tile_pool(name="const", bufs=1))
        inputs = ctx.enter_context(tc.tile_pool(name="inputs", bufs=N_CHUNKS))
        work = ctx.enter_context(tc.tile_pool(name="work", bufs=4))
        scalar_banks = ctx.enter_context(tc.psum_pool(name="scalar_banks", bufs=4))
        vector_banks = ctx.enter_context(tc.psum_pool(name="vector_banks", bufs=VECTOR_BANKS))

        ctx.enter_context(tc.manual_schedule())

        times = const.tile([P, 1], BF16)
        both_halves = const.tile([P, P], BF16)
        later_half = const.tile([P, P], BF16)
        earlier_half = const.tile([P, P], BF16)
        ones = const.tile([P, P], BF16)
        b2_row = const.tile([P, WIDTH], BF16)
        nc.vector.memset(times[:], 0.0)
        nc.vector.memset(b2_row[:], 0.0)
        nc.vector.memset(ones[:], 1.0)
        nc.vector.memset(later_half[:], 0.0)
        nc.vector.memset(later_half[0:32, :], 0.5)
        nc.vector.memset(earlier_half[:], 0.0)
        nc.vector.memset(earlier_half[32:64, :], -0.5)
        nc.vector.memset(both_halves[:], 0.5)
        unread_factor = const.tile([P, WIDTH], BF16)
        nc.gpsimd.memset(unread_factor[:], 1.0)
        identity_bf16 = const.tile([P, P], BF16)
        make_identity(nc, identity_bf16[:])

        nc.sync.dma_start(out=times[0:1, :], in_=t1.rearrange("(o n) -> o n", o=1))
        nc.sync.dma_start(out=times[32:33, :], in_=t0.rearrange("(o n) -> o n", o=1))
        w1_rows = const.tile([P, PACK, WIDTH + 2], BF16)
        w2_rows = const.tile([P, PACK, WIDTH], BF16)
        b1_cols = const.tile([P, PACK], BF16)
        h_rows = []
        k_rows = []
        for c in range(N_CHUNKS):
            h_rows.append(inputs.tile([P, slots_of(c), WIDTH], BF16, name="h_rows"))
            k_rows.append(inputs.tile([P, slots_of(c), WIDTH], BF16, name="k_rows"))
            for i, part in enumerate(parts_of(c)):
                nc.sync.dma_start(out=h_rows[c][:, part, :], in_=chunk_view(h_tilde, c)[:, part, :])
                nc.sync.dma_start(out=k_rows[c][:, part, :], in_=chunk_view(k_prev, c)[:, part, :])
                if c == 0 and i == 0:
                    nc.sync.dma_start(
                        out=w1_rows[:, :, 0 : WIDTH + 1],
                        in_=W1.rearrange("(m r) k -> m r k", r=PACK),
                    )
                    nc.sync.dma_start(out=b2_row[0:1, :], in_=b2.rearrange("(o n) -> o n", o=1))
            if c == 0:
                nc.sync.dma_start(out=b1_cols[:], in_=b1.rearrange("(m t) -> m t", t=PACK))
            if c == 2:
                nc.sync.dma_start(out=w2_rows[:], in_=W2.rearrange("(r m) k -> m r k", m=P))

        identity = const.tile([P, P], F32)
        make_identity(nc, identity[:])

        warm = const.tile([P, 1], F32)
        nc.vector.memset(warm[:], 0.0)
        nc.scalar.activation(out=warm[:], in_=warm[:], func=ACT.Tanh)

        def turn(rows, slots, grouped, word_index):
            words = rows[:].bitcast(F32)
            grouped_words = grouped[:].rearrange("p c t -> p (c t)").bitcast(F32)
            for first in range(0, slots, SLOTS_IN_BANK):
                n = min(SLOTS_IN_BANK, slots - first)
                turned = scalar_banks.tile([P, PAIRS, n * P], F32, tag="bank")
                for s in range(n):
                    for u in range(PAIRS):
                        nc.tensor.transpose(
                            turned[:, u, s * P : (s + 1) * P],
                            words[:, first + s, word_index(u)],
                            identity[:],
                        )
                nc.scalar.copy(
                    out=grouped_words[:, first * P * PAIRS : (first + n) * P * PAIRS].rearrange(
                        "p (c i u) -> p c u i", i=2, u=PAIRS
                    ),
                    in_=turned[:].rearrange("p u (c i) -> p c u i", i=2),
                )

        def halves(u):
            return slice(u * P, (u + 1) * P)

        def alternate(u):
            return slice(u, WIDTH // 2, PAIRS)

        def quantise(grouped, columns, pool, name):
            codes = pool.tile([P, columns], U32, align_bytes=64, name=name + "_codes")
            scales = pool.tile([P, columns], U8, align_bytes=64, name=name + "_scales")
            nc.vector.quantize_mx(
                out=codes[:].bitcast(FP8X4),
                scales=scales[:],
                in_=grouped[:].rearrange("p c t -> p (c t)"),
            )
            return codes, scales

        def multiply(acc, stationary, columns, moving):
            nc.tensor.matmul_mx(
                out=acc,
                lhsT=stationary[0][:, columns].bitcast(FP8X4),
                lhsT_scale=stationary[1][:, columns],
                rhs=moving[0][:].bitcast(FP8X4),
                rhs_scale=moving[1][:],
                start=True,
                stop=True,
            )

        y_rows = {}
        y_grouped = {}
        y_mx = {}
        z_planes = {}
        z_grouped = {}
        hidden = {}
        result = {}
        waiting = []

        def vector_slots(c):
            return slots_of(c) - PRODUCT_SLOTS[c]

        def combine(c, parts=None):
            if c not in y_rows:
                y_rows[c] = work.tile([P, slots_of(c), WIDTH], BF16, name="y_rows")
            for part in parts or parts_of(c):
                part = slice(part.start, min(part.stop, vector_slots(c)))
                nc.vector.scalar_tensor_tensor(
                    out=y_rows[c][:, part, :],
                    in0=k_rows[c][:, part, :],
                    scalar=spread_times[:, 0:1],
                    in1=h_rows[c][:, part, :],
                    op0=ALU.mult,
                    op1=ALU.add,
                )

        def turn_y(c):
            y_grouped[c] = work.tile(
                [P, CHUNK_ROWS[c], PACK], BF16, align_bytes=64, name="y_grouped"
            )
            for s in range(vector_slots(c), slots_of(c)):
                summed = scalar_banks.tile([P, PACK, P], F32, tag="bank")
                for t in range(PACK):
                    u, e = divmod(t, 2)
                    cols = slice(2 * P * u + e, 2 * P * (u + 1), 2)
                    terms = (
                        (h_rows[c], identity_bf16),
                        (k_rows[c], later_diagonal),
                        (k_rows[c], earlier_diagonal),
                    )
                    for i, (rows, factor) in enumerate(terms):
                        nc.tensor.matmul(
                            summed[:, t, :],
                            lhsT=rows[:, s, cols],
                            rhs=factor[:],
                            start=i == 0,
                            stop=i == len(terms) - 1,
                        )
                nc.scalar.copy(
                    out=y_grouped[c][:, s * P : (s + 1) * P, :],
                    in_=summed[:].rearrange("p t n -> p n t"),
                )
            turn(y_rows[c], vector_slots(c), y_grouped[c], halves)

        def quantise_y(c):
            y_mx[c] = quantise(y_grouped[c], CHUNK_ROWS[c], work, "y")

        def vector_cols(c):
            return int(CHUNK_ROWS[c] * Z_PART_ON_VECTOR[c])

        def gpsimd_cols(c):
            return int(CHUNK_ROWS[c] * Z_PART_ON_GPSIMD[c])

        def z_views(c, first, last):
            return (
                z_grouped[c][:, first:last, :].rearrange("p (c i) t -> p c t i", i=4),
                z_planes[c][:, :, first:last].rearrange("p t (c i) -> p c t i", i=4),
            )

        def lay_out_z(copy, c, first, last):
            laid_out, planes = z_views(c, first, last)
            copy(out=laid_out, in_=planes)

        def lay_out_z_on_gpsimd(c):
            one = work.tile([P, 1], F32, name="one")
            nc.vector.memset(one[:], 1.0)
            cols = slice(0, gpsimd_cols(c))
            nc.gpsimd.tensor_scalar(
                out=z_grouped[c][:, cols, :],
                in0=z_planes[c][:, :, cols].rearrange("p t c -> p c t"),
                scalar1=one[:, 0:1],
                scalar2=0.0,
                op0=ALU.mult,
                op1=ALU.add,
            )

        def hidden_sums(c):
            hidden[c] = []
            for r in range(PACK):
                bank = scalar_banks.tile([P, CHUNK_ROWS[c]], F32, tag="bank")
                multiply(bank[:], w1_mx, slice(r * P, (r + 1) * P), y_mx[c])
                hidden[c].append(bank)

        def hidden_tanh(c):
            rows = CHUNK_ROWS[c]
            z_planes[c] = work.tile([P, PACK, rows], BF16, name="z_planes")
            z_grouped[c] = work.tile([P, rows, PACK], BF16, align_bytes=64, name="z_grouped")
            for r in range(PACK):
                nc.scalar.activation(
                    out=z_planes[c][:, r, :],
                    in_=hidden[c][r][:],
                    func=ACT.Tanh,
                    bias=bias1[:, r : r + 1],
                )

        def finish_oldest_sum():
            c, s, summed = waiting[0]
            waiting[:] = waiting[1:]
            last = (c, s) == (N_CHUNKS - 1, slots_of(c) - 1)
            pieces = 2 if last else 1
            for i in range(pieces):
                cols = slice(i * WIDTH // pieces, (i + 1) * WIDTH // pieces)
                nc.vector.tensor_add(
                    out=result[c][:, s, cols], in0=summed[:, cols], in1=b2_all[:, cols]
                )
                nc.sync.dma_start(
                    out=chunk_view(out, c)[:, s, cols], in_=result[c][:, s, cols]
                )

        def second_layer(c):
            if vector_cols(c) > 0:
                lay_out_z(nc.vector.tensor_copy, c, gpsimd_cols(c), gpsimd_cols(c) + vector_cols(c))
            z_mx = quantise(z_grouped[c], CHUNK_ROWS[c], work, "z")
            if c + 1 < N_CHUNKS and gpsimd_cols(c + 1) > 0:
                lay_out_z_on_gpsimd(c + 1)
            result[c] = work.tile([P, slots_of(c), WIDTH], F32, name="result")
            for s in range(slots_of(c)):
                if len(waiting) == VECTOR_BANKS:
                    finish_oldest_sum()
                summed = vector_banks.tile([P, WIDTH], F32)
                multiply(summed[:], z_mx, slice(s * P, (s + 1) * P), w2_mx)
                waiting.append((c, s, summed))

        def keep_clock_up(n):
            unread = vector_banks.tile([P, WIDTH], F32, name="summed")
            for _ in range(n):
                nc.tensor.matmul(
                    unread[:], lhsT=ones[:], rhs=unread_factor[:], start=True, stop=True
                )

        spread = scalar_banks.tile([P, 4], F32, tag="bank")
        for i, factors in enumerate(
            ((later_half, earlier_half), (both_halves,), (later_half,), (earlier_half,))
        ):
            for j, factor in enumerate(factors):
                nc.tensor.matmul(
                    spread[:, i : i + 1],
                    lhsT=factor[:],
                    rhs=times[:],
                    start=j == 0,
                    stop=j == len(factors) - 1,
                )
        spread_times = const.tile([P, 4], F32)
        nc.vector.tensor_copy(out=spread_times[:], in_=spread[:])
        later_diagonal = const.tile([P, P], BF16)
        earlier_diagonal = const.tile([P, P], BF16)
        for i, diagonal in ((2, later_diagonal), (3, earlier_diagonal)):
            nc.gpsimd.tensor_scalar(
                out=diagonal[:],
                in0=identity_bf16[:],
                scalar1=spread_times[:, i : i + 1],
                scalar2=0.0,
                op0=ALU.mult,
                op1=ALU.add,
            )
        keep_clock_up(3)
        combine(0, parts_of(0)[:1])
        spread_b2 = scalar_banks.tile([P, WIDTH], F32, tag="bank")
        nc.tensor.matmul(spread_b2[:], lhsT=ones[:], rhs=b2_row[:], start=True, stop=True)
        b2_all = const.tile([P, WIDTH], F32)
        nc.vector.tensor_copy(out=b2_all[:], in_=spread_b2[:])
        combine(0, parts_of(0)[1:])
        w1_grouped = const.tile([P, WIDTH, PACK], BF16, align_bytes=64)
        turn(w1_rows, PACK, w1_grouped, halves)
        keep_clock_up(1)
        turn_y(0)
        keep_clock_up(1)
        combine(1)
        turn_y(1)
        keep_clock_up(1)
        w1_mx = quantise(w1_grouped, WIDTH, const, "w1")
        bias1 = const.tile([P, PACK], F32)
        nc.vector.scalar_tensor_tensor(
            out=bias1[:],
            in0=w1_rows[:, :, WIDTH],
            scalar=spread_times[:, 1:2],
            in1=b1_cols[:],
            op0=ALU.mult,
            op1=ALU.add,
        )

        w2_grouped = const.tile([P, WIDTH, PACK], BF16, align_bytes=64)
        quantise_y(0)
        hidden_sums(0)
        for c in range(2, Y_LEAD):
            combine(c)
        for c in range(N_CHUNKS + 1):
            if c < N_CHUNKS:
                hidden_tanh(c)
            if c + 2 < N_CHUNKS:
                turn_y(c + 2)
            if c == 0:
                turn(w2_rows, PACK, w2_grouped, alternate)
            if c + 1 < N_CHUNKS:
                quantise_y(c + 1)
            if c == 0:
                w2_mx = quantise(w2_grouped, WIDTH, const, "w2")
            if c + 1 < N_CHUNKS:
                hidden_sums(c + 1)
            if c >= 1:
                second_layer(c - 1)
            if c + Y_LEAD < N_CHUNKS:
                combine(c + Y_LEAD)
            if c < N_CHUNKS:
                lay_out_z(nc.scalar.copy, c, vector_cols(c) + gpsimd_cols(c), CHUNK_ROWS[c])
        while waiting:
            finish_oldest_sum()
